import numpy as np
import ml_dtypes


def mxq(x, axis, fmt="e4m3"):
    dtype, down = {"e4m3": (ml_dtypes.float8_e4m3fn, 7), "e5m2": (ml_dtypes.float8_e5m2, 14)}[fmt]
    v = np.moveaxis(np.asarray(x, np.float32).astype(ml_dtypes.bfloat16).astype(np.float64), axis, -1)
    blocks = v.reshape(v.shape[:-1] + (-1, 32))
    amax = np.abs(blocks).max(-1, keepdims=True)
    byte = np.maximum(np.where(amax > 0, np.frexp(amax)[1] - 1 + 127, 0) - down, 1)
    scale = np.exp2(byte - 127.0)
    codes = (blocks / scale).astype(np.float32).astype(dtype).astype(np.float64)
    return np.moveaxis((codes * scale).reshape(v.shape), -1, axis)


WIDE = False


def mx_kscale(k):
    if not WIDE:
        return np.ones(k)
    levels = np.array([10, -10, 5, -5, 0])
    a = np.random.permutation(np.resize(levels, k // 512 * 4)).reshape(k // 512, 4)
    idx = np.arange(k)
    return np.exp2(a[idx // 512, idx % 128 // 32])


BF16 = ml_dtypes.bfloat16


def bf(x):
    return np.asarray(x, np.float32).astype(BF16)


def f64(x):
    return np.asarray(x).astype(np.float64)


B, S, D, H, HD, C = 4, 2048, 1024, 1, 64, 2
DM = HD * C
EPS = 1e-9
CONST = 10000.0


def rope_tables():
    theta = 1.0 / CONST ** (np.arange(0, DM, 2) / DM)
    ang = np.arange(S)[:, None] * theta[None, :]
    return np.cos(ang), np.sin(ang)


def rope(t, cos, sin):
    tr, ti = t[..., 0::2], t[..., 1::2]
    c, s = cos[None, :, None, :], sin[None, :, None, :]
    return np.stack([tr * c - ti * s, tr * s + ti * c], axis=-1).reshape(t.shape)


def setup_inputs():
    s = mx_kscale(D)
    return {"x": bf(np.random.standard_normal((B, S, D))),
            "pre_norm_w": bf((1.0 + 0.1 * np.random.standard_normal(D)) * s),
            "wq": bf(np.random.standard_normal((H * DM, D)) / np.sqrt(D) / s[None, :]),
            "wk": bf(np.random.standard_normal((H * DM, D)) / np.sqrt(D) / s[None, :])}


def reference(x, pre_norm_w, wq, wk):
    x = f64(x)
    h = x / np.sqrt(np.mean(x * x, axis=-1, keepdims=True) + EPS) * f64(pre_norm_w)
    hq = mxq(h, 2, "e4m3")
    q = (hq @ mxq(f64(wq), 1, "e4m3").T).reshape(B, S, H, DM)
    k = (hq @ mxq(f64(wk), 1, "e4m3").T).reshape(B, S, H, DM)
    cos, sin = rope_tables()
    return rope(q, cos, sin), rope(k, cos, sin)

@@ -1,0 +1,269 @@
+import math
+from contextlib import ExitStack
+
+import concourse.mybir as mybir
+from concourse.masks import make_identity
+
+F32 = mybir.dt.float32
+BF16 = mybir.dt.bfloat16
+I32 = mybir.dt.int32
+U32 = mybir.dt.uint32
+U8 = mybir.dt.uint8
+FP8X4 = mybir.dt.float8_e4m3fn_x4
+ALU = mybir.AluOpType
+ACT = mybir.ActivationFunctionType
+
+BATCH, SEQ, D = 4, 2048, 1024
+DM = 128
+PAIRS = DM // 2
+EPS = 1e-9
+ROPE_BASE = 10000.0
+
+P = 128
+PACK = 4
+PASSES = D // (P * PACK)
+WORDS = D // 2
+SLOTS = SEQ // P
+GROUP = 4
+GROUPS_PER_SEQ = SLOTS // GROUP
+N_GROUPS = BATCH * GROUPS_PER_SEQ
+N_COLS = 4 * DM
+LOAD_AHEAD = 3
+
+ROUND_MAGIC = 12582912.0
+
+FLOPS = 2 * BATCH * SEQ * D * 2 * DM
+
+
+def tile_attention_pa_t_kernel(tc, x, pre_norm_w, wq, wk, out_0, out_1):
+    nc = tc.nc
+    x_rows = x.rearrange("b (p t) d -> b p t d", t=SLOTS)
+    out_rows = [o.rearrange("b (p t) h n -> b p (t h n)", t=SLOTS) for o in (out_0, out_1)]
+
+    with ExitStack() as ctx:
+        consts = ctx.enter_context(tc.tile_pool(name="consts", bufs=1))
+        x_pool = ctx.enter_context(tc.tile_pool(name="x", bufs=LOAD_AHEAD + 1))
+        junk = ctx.enter_context(tc.tile_pool(name="junk", bufs=2))
+        stats = ctx.enter_context(tc.tile_pool(name="stats", bufs=3))
+        h_pool = ctx.enter_context(tc.tile_pool(name="h", bufs=2))
+        grouped_pool = ctx.enter_context(tc.tile_pool(name="grouped", bufs=2))
+        mx_pool = ctx.enter_context(tc.tile_pool(name="mx", bufs=2))
+        rope_pool = ctx.enter_context(tc.tile_pool(name="rope", bufs=2))
+        out_pool = ctx.enter_context(tc.tile_pool(name="out", bufs=3))
+        psum_t = ctx.enter_context(tc.psum_pool(name="psum_t", bufs=4))
+        psum_o = ctx.enter_context(tc.psum_pool(name="psum_o", bufs=4))
+
+        x_tiles, rms_tiles, rstd_tiles = {}, {}, {}
+        grouped_tiles, code_tiles, scale_tiles = {}, {}, {}
+        acc_tiles, product_tiles = {}, {}
+
+        def load(n):
+            b, first_slot = n // GROUPS_PER_SEQ, (n % GROUPS_PER_SEQ) * GROUP
+            x_sb = x_pool.tile([P, GROUP, D], BF16)
+            nc.sync.dma_start(out=x_sb[:], in_=x_rows[b, :, first_slot : first_slot + GROUP, :])
+            x_tiles[n] = x_sb
+
+        for n in range(LOAD_AHEAD):
+            load(n)
+
+        ident = consts.tile([P, P], F32)
+        make_identity(nc, ident[:])
+
+        gain = consts.tile([P, D], BF16)
+        nc.scalar.dma_start(out=gain[:], in_=pre_norm_w.partition_broadcast(P))
+        w_rows = consts.tile([P, 2, D], BF16)
+        nc.scalar.dma_start(out=w_rows[:, 0, :], in_=wq)
+        nc.scalar.dma_start(out=w_rows[:, 1, :], in_=wk)
+
+        one = consts.tile([P, 1], F32)
+        nc.vector.memset(one[:], 1.0)
+        eps = consts.tile([P, 1], F32)
+        nc.vector.tensor_scalar(out=eps[:], in0=one[:], scalar1=EPS, scalar2=None, op0=ALU.mult)
+        quarter_turn = consts.tile([P, 1], F32)
+        nc.vector.tensor_scalar(
+            out=quarter_turn[:], in0=one[:], scalar1=math.pi / 2, scalar2=None, op0=ALU.mult
+        )
+
+        def transpose_words(words):
+            bank = psum_t.tile([P, PASSES, 2, P], F32)
+            for c in range(WORDS // P):
+                nc.tensor.transpose(bank[:, c // 2, c % 2, :], words[:, c * P : (c + 1) * P], ident[:])
+            return bank
+
+        w_grouped = consts.tile([P, PASSES, N_COLS, PACK], BF16, align_bytes=64)
+        w_grouped_words = w_grouped[:].bitcast(F32)
+        w_words = w_rows[:].bitcast(F32)
+        for m in range(2):
+            w_bank = transpose_words(w_words[:, m, :])
+            nc.vector.tensor_copy(
+                out=w_grouped_words[:, :, m * DM : (m + 1) * DM, :],
+                in_=w_bank[:].rearrange("p g u n -> p g n u"),
+            )
+            src = w_bank[:].bitcast(BF16).rearrange("p g u (j s e) -> p g s j u e", s=2, e=2)
+            dst = w_grouped[:, :, (2 + m) * DM : (3 + m) * DM, :].rearrange(
+                "p g (j s) (u e) -> p g s j u e", s=2, e=2
+            )
+            for g in range(PASSES):
+                nc.vector.tensor_scalar(
+                    out=dst[:, g, 0], in0=src[:, g, 1], scalar1=-1.0, scalar2=None, op0=ALU.mult
+                )
+                nc.vector.tensor_copy(out=dst[:, g, 1], in_=src[:, g, 0])
+        w_codes = consts.tile([P, PASSES, N_COLS], U32, align_bytes=64)
+        w_scales = consts.tile([P, PASSES, N_COLS], U8, align_bytes=64)
+        nc.vector.quantize_mx(
+            out=w_codes[:].rearrange("p g c -> p (g c)").bitcast(FP8X4),
+            scales=w_scales[:].rearrange("p g c -> p (g c)"),
+            in_=w_grouped[:].rearrange("p g c t -> p (g c t)"),
+        )
+
+        turns_per_step = consts.tile([P, PAIRS], F32)
+        for j in range(PAIRS):
+            nc.vector.tensor_scalar(
+                out=turns_per_step[:, j : j + 1],
+                in0=one[:],
+                scalar1=ROPE_BASE ** (-j / PAIRS) / (2 * math.pi),
+                scalar2=None,
+                op0=ALU.mult,
+            )
+        position_int = consts.tile([P, SLOTS], I32)
+        nc.gpsimd.iota(position_int[:], pattern=[[1, SLOTS]], base=0, channel_multiplier=SLOTS)
+        position = consts.tile([P, SLOTS], F32)
+        nc.vector.tensor_copy(out=position[:], in_=position_int[:])
+        turns = consts.tile([P, SLOTS, PAIRS], F32)
+        nc.vector.tensor_tensor(
+            out=turns[:],
+            in0=position[:].unsqueeze(2).to_broadcast([P, SLOTS, PAIRS]),
+            in1=turns_per_step[:].unsqueeze(1).to_broadcast([P, SLOTS, PAIRS]),
+            op=ALU.mult,
+        )
+        shifted = consts.tile([P, SLOTS, PAIRS], F32)
+        nc.vector.tensor_scalar(
+            out=shifted[:], in0=turns[:], scalar1=ROUND_MAGIC, scalar2=None, op0=ALU.add
+        )
+        neg_frac = consts.tile([P, SLOTS, PAIRS], F32)
+        nc.vector.scalar_tensor_tensor(
+            out=neg_frac[:], in0=shifted[:], scalar=ROUND_MAGIC, in1=turns[:],
+            op0=ALU.subtract, op1=ALU.subtract,
+        )
+        abs_frac = consts.tile([P, SLOTS, PAIRS], F32)
+        nc.vector.scalar_tensor_tensor(
+            out=abs_frac[:], in0=neg_frac[:], scalar=-1.0, in1=neg_frac[:],
+            op0=ALU.mult, op1=ALU.max,
+        )
+
+        def sum_squares(n):
+            ssq = stats.tile([P, GROUP], F32)
+            for i in range(GROUP):
+                squares = junk.tile([P, D], BF16)
+                nc.scalar.activation(
+                    out=squares[:], in_=x_tiles[n][:, i, :], func=ACT.Square,
+                    accum_out=ssq[:, i : i + 1],
+                )
+            rms = stats.tile([P, GROUP], F32)
+            nc.scalar.activation(out=rms[:], in_=ssq[:], func=ACT.Sqrt, bias=eps[:], scale=1.0 / D)
+            rms_tiles[n] = rms
+
+        def invert(n):
+            rstd = stats.tile([P, GROUP], F32)
+            nc.vector.reciprocal(out=rstd[:], in_=rms_tiles[n][:])
+            rstd_tiles[n] = rstd
+
+        sum_squares(0)
+        invert(0)
+
+        rope = consts.tile([P, SLOTS, 2, DM], F32)
+        nc.scalar.activation(
+            out=rope[:, :, 0, :].rearrange("p t (j e) -> p t j e", e=2),
+            in_=abs_frac[:].unsqueeze(3).to_broadcast([P, SLOTS, PAIRS, 2]),
+            func=ACT.Sin, bias=quarter_turn[:], scale=-2 * math.pi,
+        )
+        nc.scalar.activation(
+            out=rope[:, :, 1, :].rearrange("p t (j e) -> p t j e", e=2),
+            in_=neg_frac[:].unsqueeze(3).to_broadcast([P, SLOTS, PAIRS, 2]),
+            func=ACT.Sin, scale=-2 * math.pi,
+        )
+
+        def normalise_and_transpose(n):
+            x_sb, rstd = x_tiles[n], rstd_tiles[n]
+            h = h_pool.tile([P, GROUP, D], BF16)
+            h_words = h[:].bitcast(F32)
+            grouped = grouped_pool.tile([P, GROUP, PASSES, P, PACK], BF16, align_bytes=64)
+            grouped_words = grouped[:].bitcast(F32)
+            for i in range(GROUP):
+                nc.vector.scalar_tensor_tensor(
+                    out=h[:, i, :], in0=x_sb[:, i, :], scalar=rstd[:, i : i + 1], in1=gain[:],
+                    op0=ALU.mult, op1=ALU.mult,
+                )
+                bank = transpose_words(h_words[:, i, :])
+                nc.scalar.copy(out=grouped_words[:, i], in_=bank[:].rearrange("p g u k -> p g k u"))
+            grouped_tiles[n] = grouped
+
+        def quantise(n):
+            codes = mx_pool.tile([P, GROUP * PASSES * P], U32, align_bytes=64)
+            scales = mx_pool.tile([P, GROUP * PASSES * P], U8, align_bytes=64)
+            nc.vector.quantize_mx(
+                out=codes[:].bitcast(FP8X4),
+                scales=scales[:],
+                in_=grouped_tiles[n][:].rearrange("p i g k t -> p (i g k t)"),
+            )
+            code_tiles[n], scale_tiles[n] = codes, scales
+
+        def project(n, i):
+            acc = psum_o.tile([P, N_COLS], F32)
+            for g in range(PASSES):
+                cols = slice((i * PASSES + g) * P, (i * PASSES + g + 1) * P)
+                nc.tensor.matmul_mx(
+                    out=acc[:],
+                    lhsT=code_tiles[n][:, cols].bitcast(FP8X4),
+                    lhsT_scale=scale_tiles[n][:, cols],
+                    rhs=w_codes[:, g, :].bitcast(FP8X4),
+                    rhs_scale=w_scales[:, g, :],
+                    start=(g == 0),
+                    stop=(g == PASSES - 1),
+                )
+            acc_tiles[n, i] = acc
+
+        def rotate_products(n, i):
+            slot = (n % GROUPS_PER_SEQ) * GROUP + i
+            nc.vector.tensor_tensor(
+                out=product_tiles[n][:, i],
+                in0=acc_tiles[n, i][:].rearrange("p (c m n) -> p c m n", c=2, m=2),
+                in1=rope[:, slot].unsqueeze(2).to_broadcast([P, 2, 2, DM]),
+                op=ALU.mult,
+            )
+
+        def add_and_store(n):
+            b, first_slot = n // GROUPS_PER_SEQ, (n % GROUPS_PER_SEQ) * GROUP
+            products = product_tiles[n]
+            rotated = out_pool.tile([P, 2, GROUP, DM], F32)
+            nc.vector.tensor_tensor(
+                out=rotated[:].rearrange("p m i n -> p i m n"),
+                in0=products[:, :, 0], in1=products[:, :, 1], op=ALU.add,
+            )
+            for m in range(2):
+                nc.gpsimd.dma_start(
+                    out=out_rows[m][b, :, first_slot * DM : (first_slot + GROUP) * DM],
+                    in_=rotated[:, m].rearrange("p i n -> p (i n)"),
+                )
+
+        for step in range(N_GROUPS + 2):
+            if step + LOAD_AHEAD < N_GROUPS:
+                load(step + LOAD_AHEAD)
+            if step + 1 < N_GROUPS:
+                sum_squares(step + 1)
+            if step < N_GROUPS:
+                normalise_and_transpose(step)
+            if 1 <= step <= N_GROUPS:
+                quantise(step - 1)
+            if step >= 2:
+                products = rope_pool.tile([P, GROUP, 2, 2, DM], F32)
+                product_tiles[step - 2] = products
+            for i in range(GROUP):
+                if step >= 2:
+                    rotate_products(step - 2, i)
+                if 1 <= step <= N_GROUPS:
+                    project(step - 1, i)
+            if step >= 2:
+                add_and_store(step - 2)
+            if step + 1 < N_GROUPS:
+                invert(step + 1)

@@ -28,6 +28,8 @@ GROUP = 4
 GROUPS_PER_SEQ = SLOTS // GROUP
 N_GROUPS = BATCH * GROUPS_PER_SEQ
 N_COLS = 4 * DM
+MATMUL_COLS = 512
+GPSIMD_TILE = GROUP - 1
 LOAD_AHEAD = 3
 
 ROUND_MAGIC = 12582912.0
@@ -46,11 +48,13 @@ def tile_attention_pa_t_kernel(tc, x, pre_norm_w, wq, wk, out_0, out_1):
         junk = ctx.enter_context(tc.tile_pool(name="junk", bufs=2))
         stats = ctx.enter_context(tc.tile_pool(name="stats", bufs=3))
         h_pool = ctx.enter_context(tc.tile_pool(name="h", bufs=2))
+        weighted_pool = ctx.enter_context(tc.tile_pool(name="weighted", bufs=2))
         grouped_pool = ctx.enter_context(tc.tile_pool(name="grouped", bufs=2))
         mx_pool = ctx.enter_context(tc.tile_pool(name="mx", bufs=2))
         rope_pool = ctx.enter_context(tc.tile_pool(name="rope", bufs=2))
         out_pool = ctx.enter_context(tc.tile_pool(name="out", bufs=3))
-        psum_t = ctx.enter_context(tc.psum_pool(name="psum_t", bufs=4))
+        psum_g = ctx.enter_context(tc.psum_pool(name="psum_g", bufs=1))
+        psum_t = ctx.enter_context(tc.psum_pool(name="psum_t", bufs=3))
         psum_o = ctx.enter_context(tc.psum_pool(name="psum_o", bufs=4))
 
         x_tiles, rms_tiles, rstd_tiles = {}, {}, {}
@@ -69,8 +73,17 @@ def tile_attention_pa_t_kernel(tc, x, pre_norm_w, wq, wk, out_0, out_1):
         ident = consts.tile([P, P], F32)
         make_identity(nc, ident[:])
 
-        gain = consts.tile([P, D], BF16)
-        nc.scalar.dma_start(out=gain[:], in_=pre_norm_w.partition_broadcast(P))
+        ones = consts.tile([P, P], BF16)
+        nc.vector.memset(ones[:], 1.0)
+        gain_row = consts.tile([P, D], BF16)
+        nc.vector.memset(gain_row[:], 0.0)
+        nc.scalar.dma_start(out=gain_row[0:1, :], in_=pre_norm_w.rearrange("(o d) -> o d", o=1))
+        gain = psum_g.tile([P, D], BF16)
+        for half in range(D // MATMUL_COLS):
+            cols = slice(half * MATMUL_COLS, (half + 1) * MATMUL_COLS)
+            nc.tensor.matmul(out=gain[:, cols], lhsT=ones[:], rhs=gain_row[:, cols], start=True, stop=True)
+        gain_sb = consts.tile([P, D], BF16)
+        nc.scalar.copy(out=gain_sb[:], in_=gain[:])
         w_rows = consts.tile([P, 2, D], BF16)
         nc.scalar.dma_start(out=w_rows[:, 0, :], in_=wq)
         nc.scalar.dma_start(out=w_rows[:, 1, :], in_=wk)
@@ -189,11 +202,21 @@ def tile_attention_pa_t_kernel(tc, x, pre_norm_w, wq, wk, out_0, out_1):
             h_words = h[:].bitcast(F32)
             grouped = grouped_pool.tile([P, GROUP, PASSES, P, PACK], BF16, align_bytes=64)
             grouped_words = grouped[:].bitcast(F32)
+            weighted = weighted_pool.tile([P, D], F32)
+            nc.gpsimd.tensor_tensor(
+                out=weighted[:], in0=x_sb[:, GPSIMD_TILE, :], in1=gain_sb[:], op=ALU.mult
+            )
+            nc.gpsimd.tensor_scalar(
+                out=h[:, GPSIMD_TILE, :], in0=weighted[:],
+                scalar1=rstd[:, GPSIMD_TILE : GPSIMD_TILE + 1], scalar2=0.0,
+                op0=ALU.mult, op1=ALU.add,
+            )
             for i in range(GROUP):
-                nc.vector.scalar_tensor_tensor(
-                    out=h[:, i, :], in0=x_sb[:, i, :], scalar=rstd[:, i : i + 1], in1=gain[:],
-                    op0=ALU.mult, op1=ALU.mult,
-                )
+                if i != GPSIMD_TILE:
+                    nc.vector.scalar_tensor_tensor(
+                        out=h[:, i, :], in0=x_sb[:, i, :], scalar=rstd[:, i : i + 1], in1=gain[:],
+                        op0=ALU.mult, op1=ALU.mult,
+                    )
                 bank = transpose_words(h_words[:, i, :])
                 nc.scalar.copy(out=grouped_words[:, i], in_=bank[:].rearrange("p g u k -> p g k u"))
             grouped_tiles[n] = grouped
@@ -236,12 +259,12 @@ def tile_attention_pa_t_kernel(tc, x, pre_norm_w, wq, wk, out_0, out_1):
             b, first_slot = n // GROUPS_PER_SEQ, (n % GROUPS_PER_SEQ) * GROUP
             products = product_tiles[n]
             rotated = out_pool.tile([P, 2, GROUP, DM], F32)
-            nc.vector.tensor_tensor(
+            nc.gpsimd.tensor_tensor(
                 out=rotated[:].rearrange("p m i n -> p i m n"),
                 in0=products[:, :, 0], in1=products[:, :, 1], op=ALU.add,
             )
             for m in range(2):
-                nc.gpsimd.dma_start(
+                nc.sync.dma_start(
                     out=out_rows[m][b, :, first_slot * DM : (first_slot + GROUP) * DM],
                     in_=rotated[:, m].rearrange("p i n -> p (i n)"),
                 )

@@ -29,7 +29,6 @@ GROUPS_PER_SEQ = SLOTS // GROUP
 N_GROUPS = BATCH * GROUPS_PER_SEQ
 N_COLS = 4 * DM
 MATMUL_COLS = 512
-GPSIMD_TILE = GROUP - 1
 LOAD_AHEAD = 3
 
 ROUND_MAGIC = 12582912.0
@@ -48,7 +47,6 @@ def tile_attention_pa_t_kernel(tc, x, pre_norm_w, wq, wk, out_0, out_1):
         junk = ctx.enter_context(tc.tile_pool(name="junk", bufs=2))
         stats = ctx.enter_context(tc.tile_pool(name="stats", bufs=3))
         h_pool = ctx.enter_context(tc.tile_pool(name="h", bufs=2))
-        weighted_pool = ctx.enter_context(tc.tile_pool(name="weighted", bufs=2))
         grouped_pool = ctx.enter_context(tc.tile_pool(name="grouped", bufs=2))
         mx_pool = ctx.enter_context(tc.tile_pool(name="mx", bufs=2))
         rope_pool = ctx.enter_context(tc.tile_pool(name="rope", bufs=2))
@@ -82,8 +80,6 @@ def tile_attention_pa_t_kernel(tc, x, pre_norm_w, wq, wk, out_0, out_1):
         for half in range(D // MATMUL_COLS):
             cols = slice(half * MATMUL_COLS, (half + 1) * MATMUL_COLS)
             nc.tensor.matmul(out=gain[:, cols], lhsT=ones[:], rhs=gain_row[:, cols], start=True, stop=True)
-        gain_sb = consts.tile([P, D], BF16)
-        nc.scalar.copy(out=gain_sb[:], in_=gain[:])
         w_rows = consts.tile([P, 2, D], BF16)
         nc.scalar.dma_start(out=w_rows[:, 0, :], in_=wq)
         nc.scalar.dma_start(out=w_rows[:, 1, :], in_=wk)
@@ -202,21 +198,11 @@ def tile_attention_pa_t_kernel(tc, x, pre_norm_w, wq, wk, out_0, out_1):
             h_words = h[:].bitcast(F32)
             grouped = grouped_pool.tile([P, GROUP, PASSES, P, PACK], BF16, align_bytes=64)
             grouped_words = grouped[:].bitcast(F32)
-            weighted = weighted_pool.tile([P, D], F32)
-            nc.gpsimd.tensor_tensor(
-                out=weighted[:], in0=x_sb[:, GPSIMD_TILE, :], in1=gain_sb[:], op=ALU.mult
-            )
-            nc.gpsimd.tensor_scalar(
-                out=h[:, GPSIMD_TILE, :], in0=weighted[:],
-                scalar1=rstd[:, GPSIMD_TILE : GPSIMD_TILE + 1], scalar2=0.0,
-                op0=ALU.mult, op1=ALU.add,
-            )
             for i in range(GROUP):
-                if i != GPSIMD_TILE:
-                    nc.vector.scalar_tensor_tensor(
-                        out=h[:, i, :], in0=x_sb[:, i, :], scalar=rstd[:, i : i + 1], in1=gain[:],
-                        op0=ALU.mult, op1=ALU.mult,
-                    )
+                nc.vector.scalar_tensor_tensor(
+                    out=h[:, i, :], in0=x_sb[:, i, :], scalar=rstd[:, i : i + 1], in1=gain[:],
+                    op0=ALU.mult, op1=ALU.mult,
+                )
                 bank = transpose_words(h_words[:, i, :])
                 nc.scalar.copy(out=grouped_words[:, i], in_=bank[:].rearrange("p g u k -> p g k u"))
             grouped_tiles[n] = grouped

@@ -29,7 +29,9 @@ GROUPS_PER_SEQ = SLOTS // GROUP
 N_GROUPS = BATCH * GROUPS_PER_SEQ
 N_COLS = 4 * DM
 MATMUL_COLS = 512
-LOAD_AHEAD = 3
+GPSIMD_TILE = GROUP - 1
+STATS_AHEAD = 2
+LOAD_AHEAD = 4
 
 ROUND_MAGIC = 12582912.0
 
@@ -45,24 +47,26 @@ def tile_attention_pa_t_kernel(tc, x, pre_norm_w, wq, wk, out_0, out_1):
         consts = ctx.enter_context(tc.tile_pool(name="consts", bufs=1))
         x_pool = ctx.enter_context(tc.tile_pool(name="x", bufs=LOAD_AHEAD + 1))
         junk = ctx.enter_context(tc.tile_pool(name="junk", bufs=2))
-        stats = ctx.enter_context(tc.tile_pool(name="stats", bufs=3))
+        stats = ctx.enter_context(tc.tile_pool(name="stats", bufs=STATS_AHEAD + 2))
         h_pool = ctx.enter_context(tc.tile_pool(name="h", bufs=2))
         grouped_pool = ctx.enter_context(tc.tile_pool(name="grouped", bufs=2))
         mx_pool = ctx.enter_context(tc.tile_pool(name="mx", bufs=2))
         rope_pool = ctx.enter_context(tc.tile_pool(name="rope", bufs=2))
+        acc_pool = ctx.enter_context(tc.tile_pool(name="acc", bufs=2))
         out_pool = ctx.enter_context(tc.tile_pool(name="out", bufs=3))
         psum_g = ctx.enter_context(tc.psum_pool(name="psum_g", bufs=1))
         psum_t = ctx.enter_context(tc.psum_pool(name="psum_t", bufs=3))
         psum_o = ctx.enter_context(tc.psum_pool(name="psum_o", bufs=4))
 
-        x_tiles, rms_tiles, rstd_tiles = {}, {}, {}
+        x_tiles, rstd_tiles = {}, {}
         grouped_tiles, code_tiles, scale_tiles = {}, {}, {}
         acc_tiles, product_tiles = {}, {}
 
         def load(n):
             b, first_slot = n // GROUPS_PER_SEQ, (n % GROUPS_PER_SEQ) * GROUP
             x_sb = x_pool.tile([P, GROUP, D], BF16)
-            nc.sync.dma_start(out=x_sb[:], in_=x_rows[b, :, first_slot : first_slot + GROUP, :])
+            for i in range(GROUP):
+                nc.sync.dma_start(out=x_sb[:, i, :], in_=x_rows[b, :, first_slot + i, :])
             x_tiles[n] = x_sb
 
         for n in range(LOAD_AHEAD):
@@ -86,8 +90,10 @@ def tile_attention_pa_t_kernel(tc, x, pre_norm_w, wq, wk, out_0, out_1):
 
         one = consts.tile([P, 1], F32)
         nc.vector.memset(one[:], 1.0)
-        eps = consts.tile([P, 1], F32)
-        nc.vector.tensor_scalar(out=eps[:], in0=one[:], scalar1=EPS, scalar2=None, op0=ALU.mult)
+        minus_half = consts.tile([P, GROUP], F32)
+        nc.vector.memset(minus_half[:], -0.5)
+        warm = consts.tile([P, 1], F32)
+        nc.scalar.activation(out=warm[:], in_=one[:], func=ACT.Sin)
         quarter_turn = consts.tile([P, 1], F32)
         nc.vector.tensor_scalar(
             out=quarter_turn[:], in0=one[:], scalar1=math.pi / 2, scalar2=None, op0=ALU.mult
@@ -168,17 +174,16 @@ def tile_attention_pa_t_kernel(tc, x, pre_norm_w, wq, wk, out_0, out_1):
                     out=squares[:], in_=x_tiles[n][:, i, :], func=ACT.Square,
                     accum_out=ssq[:, i : i + 1],
                 )
-            rms = stats.tile([P, GROUP], F32)
-            nc.scalar.activation(out=rms[:], in_=ssq[:], func=ACT.Sqrt, bias=eps[:], scale=1.0 / D)
-            rms_tiles[n] = rms
-
-        def invert(n):
+            mean = stats.tile([P, GROUP], F32)
+            nc.gpsimd.tensor_scalar(
+                out=mean[:], in0=ssq[:], scalar1=1.0 / D, scalar2=EPS, op0=ALU.mult, op1=ALU.add
+            )
             rstd = stats.tile([P, GROUP], F32)
-            nc.vector.reciprocal(out=rstd[:], in_=rms_tiles[n][:])
+            nc.gpsimd.tensor_tensor(out=rstd[:], in0=mean[:], in1=minus_half[:], op=ALU.pow)
             rstd_tiles[n] = rstd
 
-        sum_squares(0)
-        invert(0)
+        for n in range(STATS_AHEAD):
+            sum_squares(n)
 
         rope = consts.tile([P, SLOTS, 2, DM], F32)
         nc.scalar.activation(
@@ -234,12 +239,21 @@ def tile_attention_pa_t_kernel(tc, x, pre_norm_w, wq, wk, out_0, out_1):
 
         def rotate_products(n, i):
             slot = (n % GROUPS_PER_SEQ) * GROUP + i
-            nc.vector.tensor_tensor(
-                out=product_tiles[n][:, i],
-                in0=acc_tiles[n, i][:].rearrange("p (c m n) -> p c m n", c=2, m=2),
-                in1=rope[:, slot].unsqueeze(2).to_broadcast([P, 2, 2, DM]),
-                op=ALU.mult,
-            )
+            table = rope[:, slot].unsqueeze(2).to_broadcast([P, 2, 2, DM])
+            if i == GPSIMD_TILE:
+                acc_sb = acc_pool.tile([P, N_COLS], F32)
+                nc.scalar.copy(out=acc_sb[:], in_=acc_tiles[n, i][:])
+                nc.gpsimd.tensor_tensor(
+                    out=product_tiles[n][:, i],
+                    in0=acc_sb[:].rearrange("p (c m n) -> p c m n", c=2, m=2),
+                    in1=table, op=ALU.mult,
+                )
+            else:
+                nc.vector.tensor_tensor(
+                    out=product_tiles[n][:, i],
+                    in0=acc_tiles[n, i][:].rearrange("p (c m n) -> p c m n", c=2, m=2),
+                    in1=table, op=ALU.mult,
+                )
 
         def add_and_store(n):
             b, first_slot = n // GROUPS_PER_SEQ, (n % GROUPS_PER_SEQ) * GROUP
@@ -258,8 +272,8 @@ def tile_attention_pa_t_kernel(tc, x, pre_norm_w, wq, wk, out_0, out_1):
         for step in range(N_GROUPS + 2):
             if step + LOAD_AHEAD < N_GROUPS:
                 load(step + LOAD_AHEAD)
-            if step + 1 < N_GROUPS:
-                sum_squares(step + 1)
+            if step + STATS_AHEAD < N_GROUPS:
+                sum_squares(step + STATS_AHEAD)
             if step < N_GROUPS:
                 normalise_and_transpose(step)
             if 1 <= step <= N_GROUPS:
@@ -274,5 +288,3 @@ def tile_attention_pa_t_kernel(tc, x, pre_norm_w, wq, wk, out_0, out_1):
                     project(step - 1, i)
             if step >= 2:
                 add_and_store(step - 2)
-            if step + 1 < N_GROUPS:
-                invert(step + 1)

@@ -58,9 +58,9 @@ def tile_attention_pa_t_kernel(tc, x, pre_norm_w, wq, wk, out_0, out_1):
         psum_t = ctx.enter_context(tc.psum_pool(name="psum_t", bufs=3))
         psum_o = ctx.enter_context(tc.psum_pool(name="psum_o", bufs=4))
 
-        x_tiles, rstd_tiles = {}, {}
+        x_tiles, ssq_tiles, rstd_tiles, h_tiles = {}, {}, {}, {}
         grouped_tiles, code_tiles, scale_tiles = {}, {}, {}
-        acc_tiles, product_tiles = {}, {}
+        acc_tiles, product_tiles, rotated_tiles = {}, {}, {}
 
         def load(n):
             b, first_slot = n // GROUPS_PER_SEQ, (n % GROUPS_PER_SEQ) * GROUP
@@ -166,24 +166,29 @@ def tile_attention_pa_t_kernel(tc, x, pre_norm_w, wq, wk, out_0, out_1):
             op0=ALU.mult, op1=ALU.max,
         )
 
-        def sum_squares(n):
-            ssq = stats.tile([P, GROUP], F32)
-            for i in range(GROUP):
-                squares = junk.tile([P, D], BF16)
-                nc.scalar.activation(
-                    out=squares[:], in_=x_tiles[n][:, i, :], func=ACT.Square,
-                    accum_out=ssq[:, i : i + 1],
-                )
+        def sum_squares(n, i):
+            squares = junk.tile([P, D], BF16)
+            nc.scalar.activation(
+                out=squares[:], in_=x_tiles[n][:, i, :], func=ACT.Square,
+                accum_out=ssq_tiles[n][:, i : i + 1],
+            )
+
+        def inverse_rms(n):
             mean = stats.tile([P, GROUP], F32)
             nc.gpsimd.tensor_scalar(
-                out=mean[:], in0=ssq[:], scalar1=1.0 / D, scalar2=EPS, op0=ALU.mult, op1=ALU.add
+                out=mean[:], in0=ssq_tiles[n][:], scalar1=1.0 / D, scalar2=EPS,
+                op0=ALU.mult, op1=ALU.add,
             )
             rstd = stats.tile([P, GROUP], F32)
             nc.gpsimd.tensor_tensor(out=rstd[:], in0=mean[:], in1=minus_half[:], op=ALU.pow)
             rstd_tiles[n] = rstd
 
         for n in range(STATS_AHEAD):
-            sum_squares(n)
+            ssq = stats.tile([P, GROUP], F32)
+            ssq_tiles[n] = ssq
+            for i in range(GROUP):
+                sum_squares(n, i)
+            inverse_rms(n)
 
         rope = consts.tile([P, SLOTS, 2, DM], F32)
         nc.scalar.activation(
@@ -197,20 +202,17 @@ def tile_attention_pa_t_kernel(tc, x, pre_norm_w, wq, wk, out_0, out_1):
             func=ACT.Sin, scale=-2 * math.pi,
         )
 
-        def normalise_and_transpose(n):
-            x_sb, rstd = x_tiles[n], rstd_tiles[n]
-            h = h_pool.tile([P, GROUP, D], BF16)
-            h_words = h[:].bitcast(F32)
-            grouped = grouped_pool.tile([P, GROUP, PASSES, P, PACK], BF16, align_bytes=64)
-            grouped_words = grouped[:].bitcast(F32)
-            for i in range(GROUP):
-                nc.vector.scalar_tensor_tensor(
-                    out=h[:, i, :], in0=x_sb[:, i, :], scalar=rstd[:, i : i + 1], in1=gain[:],
-                    op0=ALU.mult, op1=ALU.mult,
-                )
-                bank = transpose_words(h_words[:, i, :])
-                nc.scalar.copy(out=grouped_words[:, i], in_=bank[:].rearrange("p g u k -> p g k u"))
-            grouped_tiles[n] = grouped
+        def normalise_and_transpose(n, i):
+            h = h_tiles[n]
+            nc.vector.scalar_tensor_tensor(
+                out=h[:, i, :], in0=x_tiles[n][:, i, :], scalar=rstd_tiles[n][:, i : i + 1],
+                in1=gain[:], op0=ALU.mult, op1=ALU.mult,
+            )
+            bank = transpose_words(h[:].bitcast(F32)[:, i, :])
+            nc.scalar.copy(
+                out=grouped_tiles[n][:].bitcast(F32)[:, i],
+                in_=bank[:].rearrange("p g u k -> p g k u"),
+            )
 
         def quantise(n):
             codes = mx_pool.tile([P, GROUP * PASSES * P], U32, align_bytes=64)
@@ -237,12 +239,11 @@ def tile_attention_pa_t_kernel(tc, x, pre_norm_w, wq, wk, out_0, out_1):
                 )
             acc_tiles[n, i] = acc
 
-        def rotate_products(n, i):
+        def rotate(n, i):
             slot = (n % GROUPS_PER_SEQ) * GROUP + i
             table = rope[:, slot].unsqueeze(2).to_broadcast([P, 2, 2, DM])
             if i == GPSIMD_TILE:
-                acc_sb = acc_pool.tile([P, N_COLS], F32)
-                nc.scalar.copy(out=acc_sb[:], in_=acc_tiles[n, i][:])
+                acc_sb = acc_tiles[n, i]
                 nc.gpsimd.tensor_tensor(
                     out=product_tiles[n][:, i],
                     in0=acc_sb[:].rearrange("p (c m n) -> p c m n", c=2, m=2),
@@ -254,15 +255,14 @@ def tile_attention_pa_t_kernel(tc, x, pre_norm_w, wq, wk, out_0, out_1):
                     in0=acc_tiles[n, i][:].rearrange("p (c m n) -> p c m n", c=2, m=2),
                     in1=table, op=ALU.mult,
                 )
-
-        def add_and_store(n):
-            b, first_slot = n // GROUPS_PER_SEQ, (n % GROUPS_PER_SEQ) * GROUP
-            products = product_tiles[n]
-            rotated = out_pool.tile([P, 2, GROUP, DM], F32)
             nc.gpsimd.tensor_tensor(
-                out=rotated[:].rearrange("p m i n -> p i m n"),
-                in0=products[:, :, 0], in1=products[:, :, 1], op=ALU.add,
+                out=rotated_tiles[n][:, :, i, :],
+                in0=product_tiles[n][:, i, 0], in1=product_tiles[n][:, i, 1], op=ALU.add,
             )
+
+        def store(n):
+            b, first_slot = n // GROUPS_PER_SEQ, (n % GROUPS_PER_SEQ) * GROUP
+            rotated = rotated_tiles[n]
             for m in range(2):
                 nc.sync.dma_start(
                     out=out_rows[m][b, :, first_slot * DM : (first_slot + GROUP) * DM],
@@ -270,21 +270,37 @@ def tile_attention_pa_t_kernel(tc, x, pre_norm_w, wq, wk, out_0, out_1):
                 )
 
         for step in range(N_GROUPS + 2):
+            ahead, here, projected, rotating = step + STATS_AHEAD, step, step - 1, step - 2
             if step + LOAD_AHEAD < N_GROUPS:
                 load(step + LOAD_AHEAD)
-            if step + STATS_AHEAD < N_GROUPS:
-                sum_squares(step + STATS_AHEAD)
-            if step < N_GROUPS:
-                normalise_and_transpose(step)
-            if 1 <= step <= N_GROUPS:
-                quantise(step - 1)
-            if step >= 2:
-                products = rope_pool.tile([P, GROUP, 2, 2, DM], F32)
-                product_tiles[step - 2] = products
+            if rotating >= 0:
+                acc_sb = acc_pool.tile([P, N_COLS], F32)
+                nc.scalar.copy(out=acc_sb[:], in_=acc_tiles[rotating, GPSIMD_TILE][:])
+                acc_tiles[rotating, GPSIMD_TILE] = acc_sb
+            if ahead < N_GROUPS:
+                ssq = stats.tile([P, GROUP], F32)
+                ssq_tiles[ahead] = ssq
+            if here < N_GROUPS:
+                h = h_pool.tile([P, GROUP, D], BF16)
+                grouped = grouped_pool.tile([P, GROUP, PASSES, P, PACK], BF16, align_bytes=64)
+                h_tiles[here], grouped_tiles[here] = h, grouped
             for i in range(GROUP):
-                if step >= 2:
-                    rotate_products(step - 2, i)
-                if 1 <= step <= N_GROUPS:
-                    project(step - 1, i)
-            if step >= 2:
-                add_and_store(step - 2)
+                if ahead < N_GROUPS:
+                    sum_squares(ahead, i)
+                if here < N_GROUPS:
+                    normalise_and_transpose(here, i)
+            if ahead < N_GROUPS:
+                inverse_rms(ahead)
+            if 0 <= projected < N_GROUPS:
+                quantise(projected)
+            if rotating >= 0:
+                products = rope_pool.tile([P, GROUP, 2, 2, DM], F32)
+                rotated = out_pool.tile([P, 2, GROUP, DM], F32)
+                product_tiles[rotating], rotated_tiles[rotating] = products, rotated
+            for i in range(GROUP):
+                if rotating >= 0:
+                    rotate(rotating, i)
+                if 0 <= projected < N_GROUPS:
+                    project(projected, i)
+            if rotating >= 0:
+                store(rotating)

@@ -27,7 +27,8 @@ SLOTS = SEQ // P
 GROUP = 4
 GROUPS_PER_SEQ = SLOTS // GROUP
 N_GROUPS = BATCH * GROUPS_PER_SEQ
-N_COLS = 4 * DM
+N_COLS = 2 * DM
+BANK = 512
 MATMUL_COLS = 512
 GPSIMD_TILE = GROUP - 1
 STATS_AHEAD = 2
@@ -85,8 +86,10 @@ def tile_attention_pa_t_kernel(tc, x, pre_norm_w, wq, wk, out_0, out_1):
             cols = slice(half * MATMUL_COLS, (half + 1) * MATMUL_COLS)
             nc.tensor.matmul(out=gain[:, cols], lhsT=ones[:], rhs=gain_row[:, cols], start=True, stop=True)
         w_rows = consts.tile([P, 2, D], BF16)
-        nc.scalar.dma_start(out=w_rows[:, 0, :], in_=wq)
-        nc.scalar.dma_start(out=w_rows[:, 1, :], in_=wk)
+        for m, w in enumerate((wq, wk)):
+            nc.scalar.dma_start(
+                out=w_rows[m * PAIRS : (m + 1) * PAIRS, :, :], in_=w.rearrange("(j e) d -> j e d", e=2)
+            )
 
         one = consts.tile([P, 1], F32)
         nc.vector.memset(one[:], 1.0)
@@ -108,21 +111,12 @@ def tile_attention_pa_t_kernel(tc, x, pre_norm_w, wq, wk, out_0, out_1):
         w_grouped = consts.tile([P, PASSES, N_COLS, PACK], BF16, align_bytes=64)
         w_grouped_words = w_grouped[:].bitcast(F32)
         w_words = w_rows[:].bitcast(F32)
-        for m in range(2):
-            w_bank = transpose_words(w_words[:, m, :])
+        for e in range(2):
+            w_bank = transpose_words(w_words[:, e, :])
             nc.vector.tensor_copy(
-                out=w_grouped_words[:, :, m * DM : (m + 1) * DM, :],
+                out=w_grouped_words[:, :, (1 - e) * DM : (2 - e) * DM, :],
                 in_=w_bank[:].rearrange("p g u n -> p g n u"),
             )
-            src = w_bank[:].bitcast(BF16).rearrange("p g u (j s e) -> p g s j u e", s=2, e=2)
-            dst = w_grouped[:, :, (2 + m) * DM : (3 + m) * DM, :].rearrange(
-                "p g (j s) (u e) -> p g s j u e", s=2, e=2
-            )
-            for g in range(PASSES):
-                nc.vector.tensor_scalar(
-                    out=dst[:, g, 0], in0=src[:, g, 1], scalar1=-1.0, scalar2=None, op0=ALU.mult
-                )
-                nc.vector.tensor_copy(out=dst[:, g, 1], in_=src[:, g, 0])
         w_codes = consts.tile([P, PASSES, N_COLS], U32, align_bytes=64)
         w_scales = consts.tile([P, PASSES, N_COLS], U8, align_bytes=64)
         nc.vector.quantize_mx(
@@ -190,17 +184,15 @@ def tile_attention_pa_t_kernel(tc, x, pre_norm_w, wq, wk, out_0, out_1):
                 sum_squares(n, i)
             inverse_rms(n)
 
-        rope = consts.tile([P, SLOTS, 2, DM], F32)
+        rope = consts.tile([P, SLOTS, 3, PAIRS], F32)
+        cos = rope[:, :, 2, :]
+        sin = consts.tile([P, SLOTS, PAIRS], F32)
         nc.scalar.activation(
-            out=rope[:, :, 0, :].rearrange("p t (j e) -> p t j e", e=2),
-            in_=abs_frac[:].unsqueeze(3).to_broadcast([P, SLOTS, PAIRS, 2]),
-            func=ACT.Sin, bias=quarter_turn[:], scale=-2 * math.pi,
+            out=cos, in_=abs_frac[:], func=ACT.Sin, bias=quarter_turn[:], scale=-2 * math.pi
         )
-        nc.scalar.activation(
-            out=rope[:, :, 1, :].rearrange("p t (j e) -> p t j e", e=2),
-            in_=neg_frac[:].unsqueeze(3).to_broadcast([P, SLOTS, PAIRS, 2]),
-            func=ACT.Sin, scale=-2 * math.pi,
-        )
+        nc.scalar.activation(out=sin[:], in_=neg_frac[:], func=ACT.Sin, scale=-2 * math.pi)
+        nc.gpsimd.tensor_tensor(out=rope[:, :, 0, :], in0=cos, in1=sin[:], op=ALU.add)
+        nc.gpsimd.tensor_tensor(out=rope[:, :, 1, :], in0=cos, in1=sin[:], op=ALU.subtract)
 
         def normalise_and_transpose(n, i):
             h = h_tiles[n]
@@ -225,39 +217,38 @@ def tile_attention_pa_t_kernel(tc, x, pre_norm_w, wq, wk, out_0, out_1):
             code_tiles[n], scale_tiles[n] = codes, scales
 
         def project(n, i):
-            acc = psum_o.tile([P, N_COLS], F32)
-            for g in range(PASSES):
-                cols = slice((i * PASSES + g) * P, (i * PASSES + g + 1) * P)
-                nc.tensor.matmul_mx(
-                    out=acc[:],
-                    lhsT=code_tiles[n][:, cols].bitcast(FP8X4),
-                    lhsT_scale=scale_tiles[n][:, cols],
-                    rhs=w_codes[:, g, :].bitcast(FP8X4),
-                    rhs_scale=w_scales[:, g, :],
-                    start=(g == 0),
-                    stop=(g == PASSES - 1),
-                )
+            acc = psum_o.tile([P, BANK], F32)
+            members = [(0, N_COLS)], [(0, DM), (DM, N_COLS)]
+            for first_col, groups in zip((0, N_COLS), members):
+                passes = [(g, cols) for g in range(PASSES) for cols in groups]
+                for k, (g, (lo, hi)) in enumerate(passes):
+                    cols = slice((i * PASSES + g) * P, (i * PASSES + g + 1) * P)
+                    nc.tensor.matmul_mx(
+                        out=acc[:, first_col : first_col + hi - lo],
+                        lhsT=code_tiles[n][:, cols].bitcast(FP8X4),
+                        lhsT_scale=scale_tiles[n][:, cols],
+                        rhs=w_codes[:, g, lo:hi].bitcast(FP8X4),
+                        rhs_scale=w_scales[:, g, lo:hi],
+                        start=(k == 0),
+                        stop=(k == len(passes) - 1),
+                    )
             acc_tiles[n, i] = acc
 
         def rotate(n, i):
             slot = (n % GROUPS_PER_SEQ) * GROUP + i
-            table = rope[:, slot].unsqueeze(2).to_broadcast([P, 2, 2, DM])
-            if i == GPSIMD_TILE:
-                acc_sb = acc_tiles[n, i]
-                nc.gpsimd.tensor_tensor(
-                    out=product_tiles[n][:, i],
-                    in0=acc_sb[:].rearrange("p (c m n) -> p c m n", c=2, m=2),
-                    in1=table, op=ALU.mult,
-                )
-            else:
-                nc.vector.tensor_tensor(
-                    out=product_tiles[n][:, i],
-                    in0=acc_tiles[n, i][:].rearrange("p (c m n) -> p c m n", c=2, m=2),
-                    in1=table, op=ALU.mult,
-                )
+            table = rope[:, slot].unsqueeze(2).to_broadcast([P, 3, 2, PAIRS])
+            engine = nc.gpsimd if i == GPSIMD_TILE else nc.vector
+            product = product_tiles[n][:, i]
+            engine.tensor_tensor(
+                out=product,
+                in0=acc_tiles[n, i][:, : 3 * DM].rearrange("p (e m j) -> p e m j", e=3, m=2),
+                in1=table, op=ALU.mult,
+            )
             nc.gpsimd.tensor_tensor(
-                out=rotated_tiles[n][:, :, i, :],
-                in0=product_tiles[n][:, i, 0], in1=product_tiles[n][:, i, 1], op=ALU.add,
+                out=rotated_tiles[n][:, :, i, :].rearrange("p m (j e) -> p m j e", e=2),
+                in0=product[:, 2].unsqueeze(3).to_broadcast([P, 2, PAIRS, 2]),
+                in1=product[:, 0:2].rearrange("p e m j -> p m j e"),
+                op=ALU.subtract,
             )
 
         def store(n):
@@ -274,8 +265,8 @@ def tile_attention_pa_t_kernel(tc, x, pre_norm_w, wq, wk, out_0, out_1):
             if step + LOAD_AHEAD < N_GROUPS:
                 load(step + LOAD_AHEAD)
             if rotating >= 0:
-                acc_sb = acc_pool.tile([P, N_COLS], F32)
-                nc.scalar.copy(out=acc_sb[:], in_=acc_tiles[rotating, GPSIMD_TILE][:])
+                acc_sb = acc_pool.tile([P, 3 * DM], F32)
+                nc.scalar.copy(out=acc_sb[:], in_=acc_tiles[rotating, GPSIMD_TILE][:, : 3 * DM])
                 acc_tiles[rotating, GPSIMD_TILE] = acc_sb
             if ahead < N_GROUPS:
                 ssq = stats.tile([P, GROUP], F32)
@@ -294,7 +285,7 @@ def tile_attention_pa_t_kernel(tc, x, pre_norm_w, wq, wk, out_0, out_1):
             if 0 <= projected < N_GROUPS:
                 quantise(projected)
             if rotating >= 0:
-                products = rope_pool.tile([P, GROUP, 2, 2, DM], F32)
+                products = rope_pool.tile([P, GROUP, 3, 2, PAIRS], F32)
                 rotated = out_pool.tile([P, 2, GROUP, DM], F32)
                 product_tiles[rotating], rotated_tiles[rotating] = products, rotated
             for i in range(GROUP):

@@ -24,15 +24,14 @@ PACK = 4
 PASSES = D // (P * PACK)
 WORDS = D // 2
 SLOTS = SEQ // P
-GROUP = 4
-GROUPS_PER_SEQ = SLOTS // GROUP
-N_GROUPS = BATCH * GROUPS_PER_SEQ
+N_TILES = BATCH * SLOTS
 N_COLS = 2 * DM
 BANK = 512
 MATMUL_COLS = 512
-GPSIMD_TILE = GROUP - 1
+GROUP = 2
+STORE_TILES = 4
 STATS_AHEAD = 2
-LOAD_AHEAD = 4
+LOAD_AHEAD = 8
 
 ROUND_MAGIC = 12582912.0
 
@@ -43,53 +42,46 @@ def tile_attention_pa_t_kernel(tc, x, pre_norm_w, wq, wk, out_0, out_1):
     nc = tc.nc
     x_rows = x.rearrange("b (p t) d -> b p t d", t=SLOTS)
     out_rows = [o.rearrange("b (p t) h n -> b p (t h n)", t=SLOTS) for o in (out_0, out_1)]
+    groups = [[0], [1]] + [[t, t + 1] for t in range(2, N_TILES, GROUP)]
 
     with ExitStack() as ctx:
+        ctx.enter_context(tc.manual_schedule())
         consts = ctx.enter_context(tc.tile_pool(name="consts", bufs=1))
-        x_pool = ctx.enter_context(tc.tile_pool(name="x", bufs=LOAD_AHEAD + 1))
+        x_pool = ctx.enter_context(tc.tile_pool(name="x", bufs=LOAD_AHEAD + GROUP * (STATS_AHEAD + 2)))
         junk = ctx.enter_context(tc.tile_pool(name="junk", bufs=2))
-        stats = ctx.enter_context(tc.tile_pool(name="stats", bufs=STATS_AHEAD + 2))
-        h_pool = ctx.enter_context(tc.tile_pool(name="h", bufs=2))
-        grouped_pool = ctx.enter_context(tc.tile_pool(name="grouped", bufs=2))
-        mx_pool = ctx.enter_context(tc.tile_pool(name="mx", bufs=2))
-        rope_pool = ctx.enter_context(tc.tile_pool(name="rope", bufs=2))
-        acc_pool = ctx.enter_context(tc.tile_pool(name="acc", bufs=2))
+        stats = ctx.enter_context(tc.tile_pool(name="stats", bufs=STATS_AHEAD + 3))
+        h_pool = ctx.enter_context(tc.tile_pool(name="h", bufs=4))
+        mx_pool = ctx.enter_context(tc.tile_pool(name="mx", bufs=3))
+        rope_pool = ctx.enter_context(tc.tile_pool(name="rope", bufs=4))
         out_pool = ctx.enter_context(tc.tile_pool(name="out", bufs=3))
         psum_g = ctx.enter_context(tc.psum_pool(name="psum_g", bufs=1))
         psum_t = ctx.enter_context(tc.psum_pool(name="psum_t", bufs=3))
         psum_o = ctx.enter_context(tc.psum_pool(name="psum_o", bufs=4))
 
-        x_tiles, ssq_tiles, rstd_tiles, h_tiles = {}, {}, {}, {}
+        x_tiles, ssq_tiles, rstd_tiles = {}, {}, {}
         grouped_tiles, code_tiles, scale_tiles = {}, {}, {}
-        acc_tiles, product_tiles, rotated_tiles = {}, {}, {}
+        acc_tiles, rotated_tiles = {}, {}
 
-        def load(n):
-            b, first_slot = n // GROUPS_PER_SEQ, (n % GROUPS_PER_SEQ) * GROUP
-            x_sb = x_pool.tile([P, GROUP, D], BF16)
-            for i in range(GROUP):
-                nc.sync.dma_start(out=x_sb[:, i, :], in_=x_rows[b, :, first_slot + i, :])
-            x_tiles[n] = x_sb
+        def load(t):
+            x_sb = x_pool.tile([P, D], BF16)
+            nc.sync.dma_start(out=x_sb[:], in_=x_rows[t // SLOTS, :, t % SLOTS, :])
+            x_tiles[t] = x_sb
 
-        for n in range(LOAD_AHEAD):
-            load(n)
+        for t in range(LOAD_AHEAD):
+            load(t)
 
-        ident = consts.tile([P, P], F32)
-        make_identity(nc, ident[:])
-
-        ones = consts.tile([P, P], BF16)
-        nc.vector.memset(ones[:], 1.0)
         gain_row = consts.tile([P, D], BF16)
         nc.vector.memset(gain_row[:], 0.0)
         nc.scalar.dma_start(out=gain_row[0:1, :], in_=pre_norm_w.rearrange("(o d) -> o d", o=1))
-        gain = psum_g.tile([P, D], BF16)
-        for half in range(D // MATMUL_COLS):
-            cols = slice(half * MATMUL_COLS, (half + 1) * MATMUL_COLS)
-            nc.tensor.matmul(out=gain[:, cols], lhsT=ones[:], rhs=gain_row[:, cols], start=True, stop=True)
         w_rows = consts.tile([P, 2, D], BF16)
         for m, w in enumerate((wq, wk)):
             nc.scalar.dma_start(
                 out=w_rows[m * PAIRS : (m + 1) * PAIRS, :, :], in_=w.rearrange("(j e) d -> j e d", e=2)
             )
+        position_int = consts.tile([P, SLOTS], I32)
+        nc.gpsimd.iota(position_int[:], pattern=[[1, SLOTS]], base=0, channel_multiplier=SLOTS)
+        ident = consts.tile([P, P], F32)
+        make_identity(nc, ident[:])
 
         one = consts.tile([P, 1], F32)
         nc.vector.memset(one[:], 1.0)
@@ -97,10 +89,71 @@ def tile_attention_pa_t_kernel(tc, x, pre_norm_w, wq, wk, out_0, out_1):
         nc.vector.memset(minus_half[:], -0.5)
         warm = consts.tile([P, 1], F32)
         nc.scalar.activation(out=warm[:], in_=one[:], func=ACT.Sin)
+        ones = consts.tile([P, P], BF16)
+        nc.vector.memset(ones[:], 1.0)
+        gain = psum_g.tile([P, D], BF16)
+        for half in range(D // MATMUL_COLS):
+            cols = slice(half * MATMUL_COLS, (half + 1) * MATMUL_COLS)
+            nc.tensor.matmul(out=gain[:, cols], lhsT=ones[:], rhs=gain_row[:, cols], start=True, stop=True)
         quarter_turn = consts.tile([P, 1], F32)
         nc.vector.tensor_scalar(
             out=quarter_turn[:], in0=one[:], scalar1=math.pi / 2, scalar2=None, op0=ALU.mult
         )
+
+        turns_per_step = consts.tile([P, PAIRS], F32)
+        nc.vector.tensor_scalar(
+            out=turns_per_step[:, 0:1], in0=one[:], scalar1=1 / (2 * math.pi), scalar2=None, op0=ALU.mult
+        )
+        n = 1
+        while n < PAIRS:
+            nc.vector.tensor_scalar(
+                out=turns_per_step[:, n : 2 * n], in0=turns_per_step[:, 0:n],
+                scalar1=ROPE_BASE ** (-n / PAIRS), scalar2=None, op0=ALU.mult,
+            )
+            n *= 2
+        position = consts.tile([P, SLOTS], F32)
+        nc.vector.tensor_copy(out=position[:], in_=position_int[:])
+        turns = consts.tile([P, SLOTS, PAIRS], F32)
+        shifted = consts.tile([P, SLOTS, PAIRS], F32)
+        neg_frac = consts.tile([P, SLOTS, PAIRS], F32)
+        abs_frac = consts.tile([P, SLOTS, PAIRS], F32)
+        sin = consts.tile([P, SLOTS, PAIRS], F32)
+        rope = consts.tile([P, SLOTS, 3, PAIRS], F32)
+
+        def reduce_angles(lo, hi):
+            shape = [P, hi - lo, PAIRS]
+            nc.vector.tensor_tensor(
+                out=turns[:, lo:hi],
+                in0=position[:, lo:hi].unsqueeze(2).to_broadcast(shape),
+                in1=turns_per_step[:].unsqueeze(1).to_broadcast(shape),
+                op=ALU.mult,
+            )
+            nc.vector.tensor_scalar(
+                out=shifted[:, lo:hi], in0=turns[:, lo:hi], scalar1=ROUND_MAGIC, scalar2=None, op0=ALU.add
+            )
+            nc.vector.scalar_tensor_tensor(
+                out=neg_frac[:, lo:hi], in0=shifted[:, lo:hi], scalar=ROUND_MAGIC, in1=turns[:, lo:hi],
+                op0=ALU.subtract, op1=ALU.subtract,
+            )
+            nc.vector.scalar_tensor_tensor(
+                out=abs_frac[:, lo:hi], in0=neg_frac[:, lo:hi], scalar=-1.0, in1=neg_frac[:, lo:hi],
+                op0=ALU.mult, op1=ALU.max,
+            )
+
+        def make_tables(lo, hi):
+            cos = rope[:, lo:hi, 2, :]
+            nc.scalar.activation(
+                out=cos, in_=abs_frac[:, lo:hi], func=ACT.Sin, bias=quarter_turn[:], scale=-2 * math.pi
+            )
+            nc.scalar.activation(
+                out=sin[:, lo:hi], in_=neg_frac[:, lo:hi], func=ACT.Sin, scale=-2 * math.pi
+            )
+            nc.gpsimd.tensor_tensor(out=rope[:, lo:hi, 0, :], in0=cos, in1=sin[:, lo:hi], op=ALU.add)
+            nc.gpsimd.tensor_tensor(out=rope[:, lo:hi, 1, :], in0=cos, in1=sin[:, lo:hi], op=ALU.subtract)
+
+        first_slots = SLOTS // 4
+        reduce_angles(0, first_slots)
+        reduce_angles(first_slots, SLOTS)
 
         def transpose_words(words):
             bank = psum_t.tile([P, PASSES, 2, P], F32)
@@ -108,190 +161,148 @@ def tile_attention_pa_t_kernel(tc, x, pre_norm_w, wq, wk, out_0, out_1):
                 nc.tensor.transpose(bank[:, c // 2, c % 2, :], words[:, c * P : (c + 1) * P], ident[:])
             return bank
 
+        def sum_squares(t):
+            ssq = ssq_tiles[t]
+            squares = junk.tile([P, D], BF16)
+            nc.scalar.activation(out=squares[:], in_=x_tiles[t][:], func=ACT.Square, accum_out=ssq)
+
+        def start_statistics(group):
+            ssq = stats.tile([P, GROUP], F32)
+            for i, t in enumerate(group):
+                ssq_tiles[t] = ssq[:, i : i + 1]
+            return ssq
+
+        def inverse_rms(group, ssq):
+            n = len(group)
+            mean = stats.tile([P, GROUP], F32)
+            nc.gpsimd.tensor_scalar(
+                out=mean[:, :n], in0=ssq[:, :n], scalar1=1.0 / D, scalar2=EPS, op0=ALU.mult, op1=ALU.add
+            )
+            rstd = stats.tile([P, GROUP], F32)
+            nc.gpsimd.tensor_tensor(
+                out=rstd[:, :n], in0=mean[:, :n], in1=minus_half[:, :n], op=ALU.pow
+            )
+            for i, t in enumerate(group):
+                rstd_tiles[t] = rstd[:, i : i + 1]
+
+        for group in groups[:STATS_AHEAD]:
+            ssq = start_statistics(group)
+            for t in group:
+                sum_squares(t)
+            inverse_rms(group, ssq)
+
         w_grouped = consts.tile([P, PASSES, N_COLS, PACK], BF16, align_bytes=64)
         w_grouped_words = w_grouped[:].bitcast(F32)
         w_words = w_rows[:].bitcast(F32)
-        for e in range(2):
-            w_bank = transpose_words(w_words[:, e, :])
-            nc.vector.tensor_copy(
-                out=w_grouped_words[:, :, (1 - e) * DM : (2 - e) * DM, :],
-                in_=w_bank[:].rearrange("p g u n -> p g n u"),
-            )
         w_codes = consts.tile([P, PASSES, N_COLS], U32, align_bytes=64)
         w_scales = consts.tile([P, PASSES, N_COLS], U8, align_bytes=64)
+        w_banks = [transpose_words(w_words[:, e, :]) for e in range(2)]
+        for e, copy in enumerate((nc.scalar.copy, nc.vector.tensor_copy)):
+            copy(
+                out=w_grouped_words[:, :, (1 - e) * DM : (2 - e) * DM, :],
+                in_=w_banks[e][:].rearrange("p g u n -> p g n u"),
+            )
         nc.vector.quantize_mx(
             out=w_codes[:].rearrange("p g c -> p (g c)").bitcast(FP8X4),
             scales=w_scales[:].rearrange("p g c -> p (g c)"),
             in_=w_grouped[:].rearrange("p g c t -> p (g c t)"),
         )
+        make_tables(0, first_slots)
 
-        turns_per_step = consts.tile([P, PAIRS], F32)
-        for j in range(PAIRS):
-            nc.vector.tensor_scalar(
-                out=turns_per_step[:, j : j + 1],
-                in0=one[:],
-                scalar1=ROPE_BASE ** (-j / PAIRS) / (2 * math.pi),
-                scalar2=None,
-                op0=ALU.mult,
-            )
-        position_int = consts.tile([P, SLOTS], I32)
-        nc.gpsimd.iota(position_int[:], pattern=[[1, SLOTS]], base=0, channel_multiplier=SLOTS)
-        position = consts.tile([P, SLOTS], F32)
-        nc.vector.tensor_copy(out=position[:], in_=position_int[:])
-        turns = consts.tile([P, SLOTS, PAIRS], F32)
-        nc.vector.tensor_tensor(
-            out=turns[:],
-            in0=position[:].unsqueeze(2).to_broadcast([P, SLOTS, PAIRS]),
-            in1=turns_per_step[:].unsqueeze(1).to_broadcast([P, SLOTS, PAIRS]),
-            op=ALU.mult,
-        )
-        shifted = consts.tile([P, SLOTS, PAIRS], F32)
-        nc.vector.tensor_scalar(
-            out=shifted[:], in0=turns[:], scalar1=ROUND_MAGIC, scalar2=None, op0=ALU.add
-        )
-        neg_frac = consts.tile([P, SLOTS, PAIRS], F32)
-        nc.vector.scalar_tensor_tensor(
-            out=neg_frac[:], in0=shifted[:], scalar=ROUND_MAGIC, in1=turns[:],
-            op0=ALU.subtract, op1=ALU.subtract,
-        )
-        abs_frac = consts.tile([P, SLOTS, PAIRS], F32)
-        nc.vector.scalar_tensor_tensor(
-            out=abs_frac[:], in0=neg_frac[:], scalar=-1.0, in1=neg_frac[:],
-            op0=ALU.mult, op1=ALU.max,
-        )
-
-        def sum_squares(n, i):
-            squares = junk.tile([P, D], BF16)
-            nc.scalar.activation(
-                out=squares[:], in_=x_tiles[n][:, i, :], func=ACT.Square,
-                accum_out=ssq_tiles[n][:, i : i + 1],
-            )
-
-        def inverse_rms(n):
-            mean = stats.tile([P, GROUP], F32)
-            nc.gpsimd.tensor_scalar(
-                out=mean[:], in0=ssq_tiles[n][:], scalar1=1.0 / D, scalar2=EPS,
-                op0=ALU.mult, op1=ALU.add,
-            )
-            rstd = stats.tile([P, GROUP], F32)
-            nc.gpsimd.tensor_tensor(out=rstd[:], in0=mean[:], in1=minus_half[:], op=ALU.pow)
-            rstd_tiles[n] = rstd
-
-        for n in range(STATS_AHEAD):
-            ssq = stats.tile([P, GROUP], F32)
-            ssq_tiles[n] = ssq
-            for i in range(GROUP):
-                sum_squares(n, i)
-            inverse_rms(n)
-
-        rope = consts.tile([P, SLOTS, 3, PAIRS], F32)
-        cos = rope[:, :, 2, :]
-        sin = consts.tile([P, SLOTS, PAIRS], F32)
-        nc.scalar.activation(
-            out=cos, in_=abs_frac[:], func=ACT.Sin, bias=quarter_turn[:], scale=-2 * math.pi
-        )
-        nc.scalar.activation(out=sin[:], in_=neg_frac[:], func=ACT.Sin, scale=-2 * math.pi)
-        nc.gpsimd.tensor_tensor(out=rope[:, :, 0, :], in0=cos, in1=sin[:], op=ALU.add)
-        nc.gpsimd.tensor_tensor(out=rope[:, :, 1, :], in0=cos, in1=sin[:], op=ALU.subtract)
-
-        def normalise_and_transpose(n, i):
-            h = h_tiles[n]
+        def normalise_and_transpose(t, grouped, i):
+            h = h_pool.tile([P, D], BF16)
             nc.vector.scalar_tensor_tensor(
-                out=h[:, i, :], in0=x_tiles[n][:, i, :], scalar=rstd_tiles[n][:, i : i + 1],
+                out=h[:], in0=x_tiles[t][:], scalar=rstd_tiles[t],
                 in1=gain[:], op0=ALU.mult, op1=ALU.mult,
             )
-            bank = transpose_words(h[:].bitcast(F32)[:, i, :])
+            bank = transpose_words(h[:].bitcast(F32))
             nc.scalar.copy(
-                out=grouped_tiles[n][:].bitcast(F32)[:, i],
+                out=grouped[:].bitcast(F32)[:, i],
                 in_=bank[:].rearrange("p g u k -> p g k u"),
             )
 
-        def quantise(n):
+        def quantise(q):
+            n = len(groups[q]) * PASSES * P
             codes = mx_pool.tile([P, GROUP * PASSES * P], U32, align_bytes=64)
             scales = mx_pool.tile([P, GROUP * PASSES * P], U8, align_bytes=64)
             nc.vector.quantize_mx(
-                out=codes[:].bitcast(FP8X4),
-                scales=scales[:],
-                in_=grouped_tiles[n][:].rearrange("p i g k t -> p (i g k t)"),
+                out=codes[:, :n].bitcast(FP8X4),
+                scales=scales[:, :n],
+                in_=grouped_tiles[q][:].rearrange("p i g k t -> p (i g k t)")[:, : n * PACK],
             )
-            code_tiles[n], scale_tiles[n] = codes, scales
+            code_tiles[q], scale_tiles[q] = codes, scales
 
-        def project(n, i):
+        def project(q, i):
             acc = psum_o.tile([P, BANK], F32)
-            members = [(0, N_COLS)], [(0, DM), (DM, N_COLS)]
-            for first_col, groups in zip((0, N_COLS), members):
-                passes = [(g, cols) for g in range(PASSES) for cols in groups]
-                for k, (g, (lo, hi)) in enumerate(passes):
+            for first_col, windows in (0, [(0, N_COLS)]), (N_COLS, [(0, DM), (DM, N_COLS)]):
+                passes = [(g, lo, hi) for g in range(PASSES) for lo, hi in windows]
+                for k, (g, lo, hi) in enumerate(passes):
                     cols = slice((i * PASSES + g) * P, (i * PASSES + g + 1) * P)
                     nc.tensor.matmul_mx(
                         out=acc[:, first_col : first_col + hi - lo],
-                        lhsT=code_tiles[n][:, cols].bitcast(FP8X4),
-                        lhsT_scale=scale_tiles[n][:, cols],
+                        lhsT=code_tiles[q][:, cols].bitcast(FP8X4),
+                        lhsT_scale=scale_tiles[q][:, cols],
                         rhs=w_codes[:, g, lo:hi].bitcast(FP8X4),
                         rhs_scale=w_scales[:, g, lo:hi],
                         start=(k == 0),
                         stop=(k == len(passes) - 1),
                     )
-            acc_tiles[n, i] = acc
+            acc_tiles[groups[q][i]] = acc
 
-        def rotate(n, i):
-            slot = (n % GROUPS_PER_SEQ) * GROUP + i
-            table = rope[:, slot].unsqueeze(2).to_broadcast([P, 3, 2, PAIRS])
-            engine = nc.gpsimd if i == GPSIMD_TILE else nc.vector
-            product = product_tiles[n][:, i]
-            engine.tensor_tensor(
-                out=product,
-                in0=acc_tiles[n, i][:, : 3 * DM].rearrange("p (e m j) -> p e m j", e=3, m=2),
+        def rotate(t):
+            block, i = t // STORE_TILES, t % STORE_TILES
+            if i == 0:
+                rotated = out_pool.tile([P, 2, STORE_TILES, DM], F32)
+                rotated_tiles[block] = rotated
+            table = rope[:, t % SLOTS].unsqueeze(2).to_broadcast([P, 3, 2, PAIRS])
+            product = rope_pool.tile([P, 3, 2, PAIRS], F32)
+            nc.vector.tensor_tensor(
+                out=product[:],
+                in0=acc_tiles[t][:, : 3 * DM].rearrange("p (e m j) -> p e m j", e=3, m=2),
                 in1=table, op=ALU.mult,
             )
             nc.gpsimd.tensor_tensor(
-                out=rotated_tiles[n][:, :, i, :].rearrange("p m (j e) -> p m j e", e=2),
+                out=rotated_tiles[block][:, :, i, :].rearrange("p m (j e) -> p m j e", e=2),
                 in0=product[:, 2].unsqueeze(3).to_broadcast([P, 2, PAIRS, 2]),
                 in1=product[:, 0:2].rearrange("p e m j -> p m j e"),
                 op=ALU.subtract,
             )
+            n_store = STORE_TILES if t < N_TILES - STORE_TILES else GROUP
+            if (i + 1) % n_store == 0:
+                first = i + 1 - n_store
+                slot = t % SLOTS + 1 - n_store
+                for m in range(2):
+                    nc.sync.dma_start(
+                        out=out_rows[m][t // SLOTS, :, slot * DM : (slot + n_store) * DM],
+                        in_=rotated_tiles[block][:, m, first : i + 1].rearrange("p i n -> p (i n)"),
+                    )
 
-        def store(n):
-            b, first_slot = n // GROUPS_PER_SEQ, (n % GROUPS_PER_SEQ) * GROUP
-            rotated = rotated_tiles[n]
-            for m in range(2):
-                nc.sync.dma_start(
-                    out=out_rows[m][b, :, first_slot * DM : (first_slot + GROUP) * DM],
-                    in_=rotated[:, m].rearrange("p i n -> p (i n)"),
-                )
-
-        for step in range(N_GROUPS + 2):
+        loaded = LOAD_AHEAD
+        for step in range(len(groups) + 2):
             ahead, here, projected, rotating = step + STATS_AHEAD, step, step - 1, step - 2
-            if step + LOAD_AHEAD < N_GROUPS:
-                load(step + LOAD_AHEAD)
-            if rotating >= 0:
-                acc_sb = acc_pool.tile([P, 3 * DM], F32)
-                nc.scalar.copy(out=acc_sb[:], in_=acc_tiles[rotating, GPSIMD_TILE][:, : 3 * DM])
-                acc_tiles[rotating, GPSIMD_TILE] = acc_sb
-            if ahead < N_GROUPS:
-                ssq = stats.tile([P, GROUP], F32)
-                ssq_tiles[ahead] = ssq
-            if here < N_GROUPS:
-                h = h_pool.tile([P, GROUP, D], BF16)
-                grouped = grouped_pool.tile([P, GROUP, PASSES, P, PACK], BF16, align_bytes=64)
-                h_tiles[here], grouped_tiles[here] = h, grouped
+            for t in range(loaded, min(loaded + GROUP, N_TILES)):
+                load(t)
+            loaded += GROUP
+            ahead_group = groups[ahead] if ahead < len(groups) else []
+            here_group = groups[here] if here < len(groups) else []
+            if ahead_group:
+                ssq = start_statistics(ahead_group)
+            if here_group:
+                grouped = mx_pool.tile([P, GROUP, PASSES, P, PACK], BF16, align_bytes=64)
+                grouped_tiles[here] = grouped
             for i in range(GROUP):
-                if ahead < N_GROUPS:
-                    sum_squares(ahead, i)
-                if here < N_GROUPS:
-                    normalise_and_transpose(here, i)
-            if ahead < N_GROUPS:
-                inverse_rms(ahead)
-            if 0 <= projected < N_GROUPS:
+                if i < len(ahead_group):
+                    sum_squares(ahead_group[i])
+                if i < len(here_group):
+                    normalise_and_transpose(here_group[i], grouped, i)
+            if ahead_group:
+                inverse_rms(ahead_group, ssq)
+            if step == 0:
+                make_tables(first_slots, SLOTS)
+            if 0 <= projected < len(groups):
                 quantise(projected)
-            if rotating >= 0:
-                products = rope_pool.tile([P, GROUP, 3, 2, PAIRS], F32)
-                rotated = out_pool.tile([P, 2, GROUP, DM], F32)
-                product_tiles[rotating], rotated_tiles[rotating] = products, rotated
-            for i in range(GROUP):
-                if rotating >= 0:
-                    rotate(rotating, i)
-                if 0 <= projected < N_GROUPS:
+                for i in range(len(groups[projected])):
                     project(projected, i)
             if rotating >= 0:
-                store(rotating)
+                for t in groups[rotating]:
+                    rotate(t)

@@ -29,8 +29,12 @@ N_COLS = 2 * DM
 BANK = 512
 MATMUL_COLS = 512
 GROUP = 2
+SINGLES = 4
+TABLE_SLOTS = 4
+LOAD_TILES = 4
 STORE_TILES = 4
-STATS_AHEAD = 2
+GPSIMD_EVERY = 6
+STATS_AHEAD = 3
 LOAD_AHEAD = 8
 
 ROUND_MAGIC = 12582912.0
@@ -42,17 +46,21 @@ def tile_attention_pa_t_kernel(tc, x, pre_norm_w, wq, wk, out_0, out_1):
     nc = tc.nc
     x_rows = x.rearrange("b (p t) d -> b p t d", t=SLOTS)
     out_rows = [o.rearrange("b (p t) h n -> b p (t h n)", t=SLOTS) for o in (out_0, out_1)]
-    groups = [[0], [1]] + [[t, t + 1] for t in range(2, N_TILES, GROUP)]
+    last_singles = N_TILES - SINGLES // 2
+    groups = [[t] for t in range(SINGLES)]
+    groups += [[t, t + 1] for t in range(SINGLES, last_singles, GROUP)]
+    groups += [[t] for t in range(last_singles, N_TILES)]
 
     with ExitStack() as ctx:
         ctx.enter_context(tc.manual_schedule())
         consts = ctx.enter_context(tc.tile_pool(name="consts", bufs=1))
-        x_pool = ctx.enter_context(tc.tile_pool(name="x", bufs=LOAD_AHEAD + GROUP * (STATS_AHEAD + 2)))
+        x_pool = ctx.enter_context(tc.tile_pool(name="x", bufs=SINGLES + 2))
         junk = ctx.enter_context(tc.tile_pool(name="junk", bufs=2))
         stats = ctx.enter_context(tc.tile_pool(name="stats", bufs=STATS_AHEAD + 3))
         h_pool = ctx.enter_context(tc.tile_pool(name="h", bufs=4))
         mx_pool = ctx.enter_context(tc.tile_pool(name="mx", bufs=3))
-        rope_pool = ctx.enter_context(tc.tile_pool(name="rope", bufs=4))
+        rope_pool = ctx.enter_context(tc.tile_pool(name="rope", bufs=6))
+        acc_pool = ctx.enter_context(tc.tile_pool(name="acc", bufs=2))
         out_pool = ctx.enter_context(tc.tile_pool(name="out", bufs=3))
         psum_g = ctx.enter_context(tc.psum_pool(name="psum_g", bufs=1))
         psum_t = ctx.enter_context(tc.psum_pool(name="psum_t", bufs=3))
@@ -62,22 +70,26 @@ def tile_attention_pa_t_kernel(tc, x, pre_norm_w, wq, wk, out_0, out_1):
         grouped_tiles, code_tiles, scale_tiles = {}, {}, {}
         acc_tiles, rotated_tiles = {}, {}
 
-        def load(t):
-            x_sb = x_pool.tile([P, D], BF16)
-            nc.sync.dma_start(out=x_sb[:], in_=x_rows[t // SLOTS, :, t % SLOTS, :])
-            x_tiles[t] = x_sb
-
-        for t in range(LOAD_AHEAD):
-            load(t)
+        def load(first, n):
+            x_sb = x_pool.tile([P, LOAD_TILES, D], BF16)
+            slot = first % SLOTS
+            nc.sync.dma_start(out=x_sb[:, :n], in_=x_rows[first // SLOTS, :, slot : slot + n, :])
+            for i in range(n):
+                x_tiles[first + i] = x_sb[:, i, :]
 
         gain_row = consts.tile([P, D], BF16)
         nc.vector.memset(gain_row[:], 0.0)
-        nc.scalar.dma_start(out=gain_row[0:1, :], in_=pre_norm_w.rearrange("(o d) -> o d", o=1))
+        load(0, 1)
+        load(1, 1)
+        nc.sync.dma_start(out=gain_row[0:1, :], in_=pre_norm_w.rearrange("(o d) -> o d", o=1))
         w_rows = consts.tile([P, 2, D], BF16)
         for m, w in enumerate((wq, wk)):
-            nc.scalar.dma_start(
+            nc.sync.dma_start(
                 out=w_rows[m * PAIRS : (m + 1) * PAIRS, :, :], in_=w.rearrange("(j e) d -> j e d", e=2)
             )
+        load(2, 1)
+        load(3, 1)
+        load(4, LOAD_TILES)
         position_int = consts.tile([P, SLOTS], I32)
         nc.gpsimd.iota(position_int[:], pattern=[[1, SLOTS]], base=0, channel_multiplier=SLOTS)
         ident = consts.tile([P, P], F32)
@@ -101,10 +113,12 @@ def tile_attention_pa_t_kernel(tc, x, pre_norm_w, wq, wk, out_0, out_1):
         )
 
         turns_per_step = consts.tile([P, PAIRS], F32)
-        nc.vector.tensor_scalar(
-            out=turns_per_step[:, 0:1], in0=one[:], scalar1=1 / (2 * math.pi), scalar2=None, op0=ALU.mult
-        )
-        n = 1
+        n = 8
+        for j in range(n):
+            nc.vector.tensor_scalar(
+                out=turns_per_step[:, j : j + 1], in0=one[:],
+                scalar1=ROPE_BASE ** (-j / PAIRS) / (2 * math.pi), scalar2=None, op0=ALU.mult,
+            )
         while n < PAIRS:
             nc.vector.tensor_scalar(
                 out=turns_per_step[:, n : 2 * n], in0=turns_per_step[:, 0:n],
@@ -120,27 +134,33 @@ def tile_attention_pa_t_kernel(tc, x, pre_norm_w, wq, wk, out_0, out_1):
         sin = consts.tile([P, SLOTS, PAIRS], F32)
         rope = consts.tile([P, SLOTS, 3, PAIRS], F32)
 
-        def reduce_angles(lo, hi):
-            shape = [P, hi - lo, PAIRS]
-            nc.vector.tensor_tensor(
-                out=turns[:, lo:hi],
-                in0=position[:, lo:hi].unsqueeze(2).to_broadcast(shape),
-                in1=turns_per_step[:].unsqueeze(1).to_broadcast(shape),
-                op=ALU.mult,
-            )
-            nc.vector.tensor_scalar(
-                out=shifted[:, lo:hi], in0=turns[:, lo:hi], scalar1=ROUND_MAGIC, scalar2=None, op0=ALU.add
-            )
-            nc.vector.scalar_tensor_tensor(
-                out=neg_frac[:, lo:hi], in0=shifted[:, lo:hi], scalar=ROUND_MAGIC, in1=turns[:, lo:hi],
-                op0=ALU.subtract, op1=ALU.subtract,
-            )
-            nc.vector.scalar_tensor_tensor(
-                out=abs_frac[:, lo:hi], in0=neg_frac[:, lo:hi], scalar=-1.0, in1=neg_frac[:, lo:hi],
-                op0=ALU.mult, op1=ALU.max,
-            )
+        def reduce_angles(*chunks):
+            slots = [slice(c * TABLE_SLOTS, (c + 1) * TABLE_SLOTS) for c in chunks]
+            shape = [P, TABLE_SLOTS, PAIRS]
+            for s in slots:
+                nc.vector.tensor_tensor(
+                    out=turns[:, s],
+                    in0=position[:, s].unsqueeze(2).to_broadcast(shape),
+                    in1=turns_per_step[:].unsqueeze(1).to_broadcast(shape),
+                    op=ALU.mult,
+                )
+            for s in slots:
+                nc.vector.tensor_scalar(
+                    out=shifted[:, s], in0=turns[:, s], scalar1=ROUND_MAGIC, scalar2=None, op0=ALU.add
+                )
+            for s in slots:
+                nc.vector.scalar_tensor_tensor(
+                    out=neg_frac[:, s], in0=shifted[:, s], scalar=ROUND_MAGIC, in1=turns[:, s],
+                    op0=ALU.subtract, op1=ALU.subtract,
+                )
+            for s in slots:
+                nc.vector.scalar_tensor_tensor(
+                    out=abs_frac[:, s], in0=neg_frac[:, s], scalar=-1.0, in1=neg_frac[:, s],
+                    op0=ALU.mult, op1=ALU.max,
+                )
 
-        def make_tables(lo, hi):
+        def make_table(chunk):
+            lo, hi = chunk * TABLE_SLOTS, (chunk + 1) * TABLE_SLOTS
             cos = rope[:, lo:hi, 2, :]
             nc.scalar.activation(
                 out=cos, in_=abs_frac[:, lo:hi], func=ACT.Sin, bias=quarter_turn[:], scale=-2 * math.pi
@@ -151,9 +171,7 @@ def tile_attention_pa_t_kernel(tc, x, pre_norm_w, wq, wk, out_0, out_1):
             nc.gpsimd.tensor_tensor(out=rope[:, lo:hi, 0, :], in0=cos, in1=sin[:, lo:hi], op=ALU.add)
             nc.gpsimd.tensor_tensor(out=rope[:, lo:hi, 1, :], in0=cos, in1=sin[:, lo:hi], op=ALU.subtract)
 
-        first_slots = SLOTS // 4
-        reduce_angles(0, first_slots)
-        reduce_angles(first_slots, SLOTS)
+        reduce_angles(0, 1)
 
         def transpose_words(words):
             bank = psum_t.tile([P, PASSES, 2, P], F32)
@@ -164,7 +182,7 @@ def tile_attention_pa_t_kernel(tc, x, pre_norm_w, wq, wk, out_0, out_1):
         def sum_squares(t):
             ssq = ssq_tiles[t]
             squares = junk.tile([P, D], BF16)
-            nc.scalar.activation(out=squares[:], in_=x_tiles[t][:], func=ACT.Square, accum_out=ssq)
+            nc.scalar.activation(out=squares[:], in_=x_tiles[t], func=ACT.Square, accum_out=ssq)
 
         def start_statistics(group):
             ssq = stats.tile([P, GROUP], F32)
@@ -197,22 +215,23 @@ def tile_attention_pa_t_kernel(tc, x, pre_norm_w, wq, wk, out_0, out_1):
         w_codes = consts.tile([P, PASSES, N_COLS], U32, align_bytes=64)
         w_scales = consts.tile([P, PASSES, N_COLS], U8, align_bytes=64)
         w_banks = [transpose_words(w_words[:, e, :]) for e in range(2)]
-        for e, copy in enumerate((nc.scalar.copy, nc.vector.tensor_copy)):
-            copy(
-                out=w_grouped_words[:, :, (1 - e) * DM : (2 - e) * DM, :],
-                in_=w_banks[e][:].rearrange("p g u n -> p g n u"),
+
+        def prepare_weights():
+            for e, w_bank in enumerate(w_banks):
+                nc.vector.tensor_copy(
+                    out=w_grouped_words[:, :, (1 - e) * DM : (2 - e) * DM, :],
+                    in_=w_bank[:].rearrange("p g u n -> p g n u"),
+                )
+            nc.vector.quantize_mx(
+                out=w_codes[:].rearrange("p g c -> p (g c)").bitcast(FP8X4),
+                scales=w_scales[:].rearrange("p g c -> p (g c)"),
+                in_=w_grouped[:].rearrange("p g c t -> p (g c t)"),
             )
-        nc.vector.quantize_mx(
-            out=w_codes[:].rearrange("p g c -> p (g c)").bitcast(FP8X4),
-            scales=w_scales[:].rearrange("p g c -> p (g c)"),
-            in_=w_grouped[:].rearrange("p g c t -> p (g c t)"),
-        )
-        make_tables(0, first_slots)
 
         def normalise_and_transpose(t, grouped, i):
             h = h_pool.tile([P, D], BF16)
             nc.vector.scalar_tensor_tensor(
-                out=h[:], in0=x_tiles[t][:], scalar=rstd_tiles[t],
+                out=h[:], in0=x_tiles[t], scalar=rstd_tiles[t],
                 in1=gain[:], op0=ALU.mult, op1=ALU.mult,
             )
             bank = transpose_words(h[:].bitcast(F32))
@@ -249,42 +268,57 @@ def tile_attention_pa_t_kernel(tc, x, pre_norm_w, wq, wk, out_0, out_1):
                     )
             acc_tiles[groups[q][i]] = acc
 
+        def on_gpsimd(t):
+            return t % GPSIMD_EVERY == GPSIMD_EVERY - 1 and SINGLES <= t < last_singles
+
+        def copy_for_gpsimd(t):
+            acc_sb = acc_pool.tile([P, 3 * DM], F32)
+            nc.scalar.copy(out=acc_sb[:], in_=acc_tiles[t][:, : 3 * DM])
+            acc_tiles[t] = acc_sb
+
         def rotate(t):
-            block, i = t // STORE_TILES, t % STORE_TILES
+            last = t >= last_singles
+            n_store = 1 if last else GROUP if t >= N_TILES - STORE_TILES else STORE_TILES
+            i = t % n_store
             if i == 0:
                 rotated = out_pool.tile([P, 2, STORE_TILES, DM], F32)
-                rotated_tiles[block] = rotated
+            else:
+                rotated = rotated_tiles[t - 1]
+            rotated_tiles[t] = rotated
             table = rope[:, t % SLOTS].unsqueeze(2).to_broadcast([P, 3, 2, PAIRS])
             product = rope_pool.tile([P, 3, 2, PAIRS], F32)
-            nc.vector.tensor_tensor(
+            engine = nc.gpsimd if on_gpsimd(t) else nc.vector
+            engine.tensor_tensor(
                 out=product[:],
                 in0=acc_tiles[t][:, : 3 * DM].rearrange("p (e m j) -> p e m j", e=3, m=2),
                 in1=table, op=ALU.mult,
             )
-            nc.gpsimd.tensor_tensor(
-                out=rotated_tiles[block][:, :, i, :].rearrange("p m (j e) -> p m j e", e=2),
+            (nc.vector if last else nc.gpsimd).tensor_tensor(
+                out=rotated[:, :, i, :].rearrange("p m (j e) -> p m j e", e=2),
                 in0=product[:, 2].unsqueeze(3).to_broadcast([P, 2, PAIRS, 2]),
                 in1=product[:, 0:2].rearrange("p e m j -> p m j e"),
                 op=ALU.subtract,
             )
-            n_store = STORE_TILES if t < N_TILES - STORE_TILES else GROUP
-            if (i + 1) % n_store == 0:
-                first = i + 1 - n_store
-                slot = t % SLOTS + 1 - n_store
+            if i + 1 == n_store:
+                slot = t % SLOTS - i
                 for m in range(2):
                     nc.sync.dma_start(
                         out=out_rows[m][t // SLOTS, :, slot * DM : (slot + n_store) * DM],
-                        in_=rotated_tiles[block][:, m, first : i + 1].rearrange("p i n -> p (i n)"),
+                        in_=rotated[:, m, :n_store].rearrange("p i n -> p (i n)"),
                     )
 
-        loaded = LOAD_AHEAD
+        loaded = SINGLES + LOAD_TILES
         for step in range(len(groups) + 2):
             ahead, here, projected, rotating = step + STATS_AHEAD, step, step - 1, step - 2
-            for t in range(loaded, min(loaded + GROUP, N_TILES)):
-                load(t)
-            loaded += GROUP
             ahead_group = groups[ahead] if ahead < len(groups) else []
             here_group = groups[here] if here < len(groups) else []
+            if here_group and loaded < min(here_group[0] + LOAD_AHEAD + LOAD_TILES, N_TILES):
+                load(loaded, LOAD_TILES)
+                loaded += LOAD_TILES
+            if rotating >= 0:
+                for t in groups[rotating]:
+                    if on_gpsimd(t):
+                        copy_for_gpsimd(t)
             if ahead_group:
                 ssq = start_statistics(ahead_group)
             if here_group:
@@ -298,7 +332,13 @@ def tile_attention_pa_t_kernel(tc, x, pre_norm_w, wq, wk, out_0, out_1):
             if ahead_group:
                 inverse_rms(ahead_group, ssq)
             if step == 0:
-                make_tables(first_slots, SLOTS)
+                make_table(0)
+                prepare_weights()
+            if step == 1:
+                make_table(1)
+                reduce_angles(2, 3)
+            if step in (4, 6):
+                make_table(step // 2)
             if 0 <= projected < len(groups):
                 quantise(projected)
                 for i in range(len(groups[projected])):

@@ -28,12 +28,11 @@ N_TILES = BATCH * SLOTS
 N_COLS = 2 * DM
 BANK = 512
 MATMUL_COLS = 512
-GROUP = 2
+STATS_TILES = 2
 SINGLES = 4
 TABLE_SLOTS = 4
 LOAD_TILES = 4
 STORE_TILES = 4
-GPSIMD_EVERY = 6
 STATS_AHEAD = 3
 LOAD_AHEAD = 8
 
@@ -46,21 +45,15 @@ def tile_attention_pa_t_kernel(tc, x, pre_norm_w, wq, wk, out_0, out_1):
     nc = tc.nc
     x_rows = x.rearrange("b (p t) d -> b p t d", t=SLOTS)
     out_rows = [o.rearrange("b (p t) h n -> b p (t h n)", t=SLOTS) for o in (out_0, out_1)]
-    last_singles = N_TILES - SINGLES // 2
-    groups = [[t] for t in range(SINGLES)]
-    groups += [[t, t + 1] for t in range(SINGLES, last_singles, GROUP)]
-    groups += [[t] for t in range(last_singles, N_TILES)]
-
     with ExitStack() as ctx:
         ctx.enter_context(tc.manual_schedule())
         consts = ctx.enter_context(tc.tile_pool(name="consts", bufs=1))
         x_pool = ctx.enter_context(tc.tile_pool(name="x", bufs=SINGLES + 2))
         junk = ctx.enter_context(tc.tile_pool(name="junk", bufs=2))
-        stats = ctx.enter_context(tc.tile_pool(name="stats", bufs=STATS_AHEAD + 3))
+        stats = ctx.enter_context(tc.tile_pool(name="stats", bufs=STATS_AHEAD + 2))
         h_pool = ctx.enter_context(tc.tile_pool(name="h", bufs=4))
-        mx_pool = ctx.enter_context(tc.tile_pool(name="mx", bufs=3))
+        mx_pool = ctx.enter_context(tc.tile_pool(name="mx", bufs=4))
         rope_pool = ctx.enter_context(tc.tile_pool(name="rope", bufs=6))
-        acc_pool = ctx.enter_context(tc.tile_pool(name="acc", bufs=2))
         out_pool = ctx.enter_context(tc.tile_pool(name="out", bufs=3))
         psum_g = ctx.enter_context(tc.psum_pool(name="psum_g", bufs=1))
         psum_t = ctx.enter_context(tc.psum_pool(name="psum_t", bufs=3))
@@ -97,7 +90,7 @@ def tile_attention_pa_t_kernel(tc, x, pre_norm_w, wq, wk, out_0, out_1):
 
         one = consts.tile([P, 1], F32)
         nc.vector.memset(one[:], 1.0)
-        minus_half = consts.tile([P, GROUP], F32)
+        minus_half = consts.tile([P, STATS_TILES], F32)
         nc.vector.memset(minus_half[:], -0.5)
         warm = consts.tile([P, 1], F32)
         nc.scalar.activation(out=warm[:], in_=one[:], func=ACT.Sin)
@@ -180,34 +173,32 @@ def tile_attention_pa_t_kernel(tc, x, pre_norm_w, wq, wk, out_0, out_1):
             return bank
 
         def sum_squares(t):
-            ssq = ssq_tiles[t]
+            n = 1 if t < SINGLES else STATS_TILES
+            i = t % n
+            if i == 0:
+                ssq = stats.tile([P, STATS_TILES], F32)
+            else:
+                ssq = ssq_tiles[t - 1]
+            ssq_tiles[t] = ssq
             squares = junk.tile([P, D], BF16)
-            nc.scalar.activation(out=squares[:], in_=x_tiles[t], func=ACT.Square, accum_out=ssq)
-
-        def start_statistics(group):
-            ssq = stats.tile([P, GROUP], F32)
-            for i, t in enumerate(group):
-                ssq_tiles[t] = ssq[:, i : i + 1]
-            return ssq
-
-        def inverse_rms(group, ssq):
-            n = len(group)
-            mean = stats.tile([P, GROUP], F32)
-            nc.gpsimd.tensor_scalar(
-                out=mean[:, :n], in0=ssq[:, :n], scalar1=1.0 / D, scalar2=EPS, op0=ALU.mult, op1=ALU.add
+            nc.scalar.activation(
+                out=squares[:], in_=x_tiles[t], func=ACT.Square, accum_out=ssq[:, i : i + 1]
             )
-            rstd = stats.tile([P, GROUP], F32)
-            nc.gpsimd.tensor_tensor(
-                out=rstd[:, :n], in0=mean[:, :n], in1=minus_half[:, :n], op=ALU.pow
-            )
-            for i, t in enumerate(group):
-                rstd_tiles[t] = rstd[:, i : i + 1]
+            if i + 1 == n:
+                mean = stats.tile([P, STATS_TILES], F32)
+                nc.gpsimd.tensor_scalar(
+                    out=mean[:, :n], in0=ssq[:, :n], scalar1=1.0 / D, scalar2=EPS,
+                    op0=ALU.mult, op1=ALU.add,
+                )
+                rstd = stats.tile([P, STATS_TILES], F32)
+                nc.gpsimd.tensor_tensor(
+                    out=rstd[:, :n], in0=mean[:, :n], in1=minus_half[:, :n], op=ALU.pow
+                )
+                for k in range(n):
+                    rstd_tiles[t + 1 - n + k] = rstd[:, k : k + 1]
 
-        for group in groups[:STATS_AHEAD]:
-            ssq = start_statistics(group)
-            for t in group:
-                sum_squares(t)
-            inverse_rms(group, ssq)
+        for t in range(STATS_AHEAD):
+            sum_squares(t)
 
         w_grouped = consts.tile([P, PASSES, N_COLS, PACK], BF16, align_bytes=64)
         w_grouped_words = w_grouped[:].bitcast(F32)
@@ -228,57 +219,49 @@ def tile_attention_pa_t_kernel(tc, x, pre_norm_w, wq, wk, out_0, out_1):
                 in_=w_grouped[:].rearrange("p g c t -> p (g c t)"),
             )
 
-        def normalise_and_transpose(t, grouped, i):
+        def normalise_and_transpose(t):
             h = h_pool.tile([P, D], BF16)
             nc.vector.scalar_tensor_tensor(
                 out=h[:], in0=x_tiles[t], scalar=rstd_tiles[t],
                 in1=gain[:], op0=ALU.mult, op1=ALU.mult,
             )
             bank = transpose_words(h[:].bitcast(F32))
+            grouped = mx_pool.tile([P, PASSES, P, PACK], BF16, align_bytes=64)
             nc.scalar.copy(
-                out=grouped[:].bitcast(F32)[:, i],
+                out=grouped[:].bitcast(F32),
                 in_=bank[:].rearrange("p g u k -> p g k u"),
             )
+            grouped_tiles[t] = grouped
 
-        def quantise(q):
-            n = len(groups[q]) * PASSES * P
-            codes = mx_pool.tile([P, GROUP * PASSES * P], U32, align_bytes=64)
-            scales = mx_pool.tile([P, GROUP * PASSES * P], U8, align_bytes=64)
+        def quantise(t):
+            codes = mx_pool.tile([P, PASSES, P], U32, align_bytes=64)
+            scales = mx_pool.tile([P, PASSES, P], U8, align_bytes=64)
             nc.vector.quantize_mx(
-                out=codes[:, :n].bitcast(FP8X4),
-                scales=scales[:, :n],
-                in_=grouped_tiles[q][:].rearrange("p i g k t -> p (i g k t)")[:, : n * PACK],
+                out=codes[:].rearrange("p g k -> p (g k)").bitcast(FP8X4),
+                scales=scales[:].rearrange("p g k -> p (g k)"),
+                in_=grouped_tiles[t][:].rearrange("p g k t -> p (g k t)"),
             )
-            code_tiles[q], scale_tiles[q] = codes, scales
+            code_tiles[t], scale_tiles[t] = codes, scales
 
-        def project(q, i):
+        def project(t):
             acc = psum_o.tile([P, BANK], F32)
             for first_col, windows in (0, [(0, N_COLS)]), (N_COLS, [(0, DM), (DM, N_COLS)]):
                 passes = [(g, lo, hi) for g in range(PASSES) for lo, hi in windows]
                 for k, (g, lo, hi) in enumerate(passes):
-                    cols = slice((i * PASSES + g) * P, (i * PASSES + g + 1) * P)
                     nc.tensor.matmul_mx(
                         out=acc[:, first_col : first_col + hi - lo],
-                        lhsT=code_tiles[q][:, cols].bitcast(FP8X4),
-                        lhsT_scale=scale_tiles[q][:, cols],
+                        lhsT=code_tiles[t][:, g, :].bitcast(FP8X4),
+                        lhsT_scale=scale_tiles[t][:, g, :],
                         rhs=w_codes[:, g, lo:hi].bitcast(FP8X4),
                         rhs_scale=w_scales[:, g, lo:hi],
                         start=(k == 0),
                         stop=(k == len(passes) - 1),
                     )
-            acc_tiles[groups[q][i]] = acc
-
-        def on_gpsimd(t):
-            return t % GPSIMD_EVERY == GPSIMD_EVERY - 1 and SINGLES <= t < last_singles
-
-        def copy_for_gpsimd(t):
-            acc_sb = acc_pool.tile([P, 3 * DM], F32)
-            nc.scalar.copy(out=acc_sb[:], in_=acc_tiles[t][:, : 3 * DM])
-            acc_tiles[t] = acc_sb
+            acc_tiles[t] = acc
 
         def rotate(t):
-            last = t >= last_singles
-            n_store = 1 if last else GROUP if t >= N_TILES - STORE_TILES else STORE_TILES
+            last = t >= N_TILES - STORE_TILES // 2
+            n_store = 1 if last else 2 if t >= N_TILES - STORE_TILES else STORE_TILES
             i = t % n_store
             if i == 0:
                 rotated = out_pool.tile([P, 2, STORE_TILES, DM], F32)
@@ -287,8 +270,7 @@ def tile_attention_pa_t_kernel(tc, x, pre_norm_w, wq, wk, out_0, out_1):
             rotated_tiles[t] = rotated
             table = rope[:, t % SLOTS].unsqueeze(2).to_broadcast([P, 3, 2, PAIRS])
             product = rope_pool.tile([P, 3, 2, PAIRS], F32)
-            engine = nc.gpsimd if on_gpsimd(t) else nc.vector
-            engine.tensor_tensor(
+            nc.vector.tensor_tensor(
                 out=product[:],
                 in0=acc_tiles[t][:, : 3 * DM].rearrange("p (e m j) -> p e m j", e=3, m=2),
                 in1=table, op=ALU.mult,
@@ -308,41 +290,24 @@ def tile_attention_pa_t_kernel(tc, x, pre_norm_w, wq, wk, out_0, out_1):
                     )
 
         loaded = SINGLES + LOAD_TILES
-        for step in range(len(groups) + 2):
-            ahead, here, projected, rotating = step + STATS_AHEAD, step, step - 1, step - 2
-            ahead_group = groups[ahead] if ahead < len(groups) else []
-            here_group = groups[here] if here < len(groups) else []
-            if here_group and loaded < min(here_group[0] + LOAD_AHEAD + LOAD_TILES, N_TILES):
+        for step in range(N_TILES + 2):
+            if loaded < min(step + LOAD_AHEAD + LOAD_TILES, N_TILES):
                 load(loaded, LOAD_TILES)
                 loaded += LOAD_TILES
-            if rotating >= 0:
-                for t in groups[rotating]:
-                    if on_gpsimd(t):
-                        copy_for_gpsimd(t)
-            if ahead_group:
-                ssq = start_statistics(ahead_group)
-            if here_group:
-                grouped = mx_pool.tile([P, GROUP, PASSES, P, PACK], BF16, align_bytes=64)
-                grouped_tiles[here] = grouped
-            for i in range(GROUP):
-                if i < len(ahead_group):
-                    sum_squares(ahead_group[i])
-                if i < len(here_group):
-                    normalise_and_transpose(here_group[i], grouped, i)
-            if ahead_group:
-                inverse_rms(ahead_group, ssq)
+            if step + STATS_AHEAD < N_TILES:
+                sum_squares(step + STATS_AHEAD)
+            if step < N_TILES:
+                normalise_and_transpose(step)
             if step == 0:
                 make_table(0)
                 prepare_weights()
             if step == 1:
                 make_table(1)
                 reduce_angles(2, 3)
-            if step in (4, 6):
-                make_table(step // 2)
-            if 0 <= projected < len(groups):
-                quantise(projected)
-                for i in range(len(groups[projected])):
-                    project(projected, i)
-            if rotating >= 0:
-                for t in groups[rotating]:
-                    rotate(t)
+            if step in (4, 8):
+                make_table(step // 4 + 1)
+            if 0 <= step - 1 < N_TILES:
+                quantise(step - 1)
+                project(step - 1)
+            if step >= 2:
+                rotate(step - 2)

@@ -34,6 +34,8 @@ TABLE_SLOTS = 4
 LOAD_TILES = 4
 STORE_TILES = 4
 STATS_AHEAD = 3
+PROJECT_BEHIND = 2
+ROTATE_BEHIND = 3
 LOAD_AHEAD = 8
 
 ROUND_MAGIC = 12582912.0
@@ -166,8 +168,10 @@ def tile_attention_pa_t_kernel(tc, x, pre_norm_w, wq, wk, out_0, out_1):
 
         reduce_angles(0, 1)
 
-        def transpose_words(words):
+        def transpose_words(words, warm_up=False):
             bank = psum_t.tile([P, PASSES, 2, P], F32)
+            if warm_up:
+                nc.tensor.matmul(out=bank[:, 0, 0, :], lhsT=ones[:], rhs=ones[:], start=True, stop=True)
             for c in range(WORDS // P):
                 nc.tensor.transpose(bank[:, c // 2, c % 2, :], words[:, c * P : (c + 1) * P], ident[:])
             return bank
@@ -225,7 +229,7 @@ def tile_attention_pa_t_kernel(tc, x, pre_norm_w, wq, wk, out_0, out_1):
                 out=h[:], in0=x_tiles[t], scalar=rstd_tiles[t],
                 in1=gain[:], op0=ALU.mult, op1=ALU.mult,
             )
-            bank = transpose_words(h[:].bitcast(F32))
+            bank = transpose_words(h[:].bitcast(F32), warm_up=True)
             grouped = mx_pool.tile([P, PASSES, P, PACK], BF16, align_bytes=64)
             nc.scalar.copy(
                 out=grouped[:].bitcast(F32),
@@ -290,6 +294,7 @@ def tile_attention_pa_t_kernel(tc, x, pre_norm_w, wq, wk, out_0, out_1):
                     )
 
         loaded = SINGLES + LOAD_TILES
+        next_projected, next_rotated = 0, 0
         for step in range(N_TILES + 2):
             if loaded < min(step + LOAD_AHEAD + LOAD_TILES, N_TILES):
                 load(loaded, LOAD_TILES)
@@ -306,8 +311,11 @@ def tile_attention_pa_t_kernel(tc, x, pre_norm_w, wq, wk, out_0, out_1):
                 reduce_angles(2, 3)
             if step in (4, 8):
                 make_table(step // 4 + 1)
-            if 0 <= step - 1 < N_TILES:
-                quantise(step - 1)
-                project(step - 1)
-            if step >= 2:
-                rotate(step - 2)
+            catch_up = 1 if step >= N_TILES - 1 else 0
+            while next_projected <= min(step - PROJECT_BEHIND + catch_up, N_TILES - 1):
+                quantise(next_projected)
+                project(next_projected)
+                next_projected += 1
+            while next_rotated <= step - ROTATE_BEHIND + catch_up:
+                rotate(next_rotated)
+                next_rotated += 1

@@ -33,6 +33,8 @@ SINGLES = 4
 TABLE_SLOTS = 4
 LOAD_TILES = 4
 STORE_TILES = 4
+FIRST_SCALAR_RSTD = 6
+GPSIMD_EVERY = 8
 STATS_AHEAD = 3
 PROJECT_BEHIND = 2
 ROTATE_BEHIND = 3
@@ -56,6 +58,7 @@ def tile_attention_pa_t_kernel(tc, x, pre_norm_w, wq, wk, out_0, out_1):
         h_pool = ctx.enter_context(tc.tile_pool(name="h", bufs=4))
         mx_pool = ctx.enter_context(tc.tile_pool(name="mx", bufs=4))
         rope_pool = ctx.enter_context(tc.tile_pool(name="rope", bufs=6))
+        acc_pool = ctx.enter_context(tc.tile_pool(name="acc", bufs=2))
         out_pool = ctx.enter_context(tc.tile_pool(name="out", bufs=3))
         psum_g = ctx.enter_context(tc.psum_pool(name="psum_g", bufs=1))
         psum_t = ctx.enter_context(tc.psum_pool(name="psum_t", bufs=3))
@@ -102,6 +105,8 @@ def tile_attention_pa_t_kernel(tc, x, pre_norm_w, wq, wk, out_0, out_1):
         for half in range(D // MATMUL_COLS):
             cols = slice(half * MATMUL_COLS, (half + 1) * MATMUL_COLS)
             nc.tensor.matmul(out=gain[:, cols], lhsT=ones[:], rhs=gain_row[:, cols], start=True, stop=True)
+        eps = consts.tile([P, 1], F32)
+        nc.vector.tensor_scalar(out=eps[:], in0=one[:], scalar1=EPS, scalar2=None, op0=ALU.mult)
         quarter_turn = consts.tile([P, 1], F32)
         nc.vector.tensor_scalar(
             out=quarter_turn[:], in0=one[:], scalar1=math.pi / 2, scalar2=None, op0=ALU.mult
@@ -168,10 +173,8 @@ def tile_attention_pa_t_kernel(tc, x, pre_norm_w, wq, wk, out_0, out_1):
 
         reduce_angles(0, 1)
 
-        def transpose_words(words, warm_up=False):
+        def transpose_words(words):
             bank = psum_t.tile([P, PASSES, 2, P], F32)
-            if warm_up:
-                nc.tensor.matmul(out=bank[:, 0, 0, :], lhsT=ones[:], rhs=ones[:], start=True, stop=True)
             for c in range(WORDS // P):
                 nc.tensor.transpose(bank[:, c // 2, c % 2, :], words[:, c * P : (c + 1) * P], ident[:])
             return bank
@@ -188,18 +191,25 @@ def tile_attention_pa_t_kernel(tc, x, pre_norm_w, wq, wk, out_0, out_1):
             nc.scalar.activation(
                 out=squares[:], in_=x_tiles[t], func=ACT.Square, accum_out=ssq[:, i : i + 1]
             )
-            if i + 1 == n:
+            if i + 1 < n:
+                return
+            rstd = stats.tile([P, STATS_TILES], F32)
+            if t >= FIRST_SCALAR_RSTD:
+                nc.scalar.activation(
+                    out=rstd[:, :n], in_=ssq[:, :n], func=ACT.Abs_reciprocal_sqrt,
+                    bias=eps[:], scale=1.0 / D,
+                )
+            else:
                 mean = stats.tile([P, STATS_TILES], F32)
                 nc.gpsimd.tensor_scalar(
                     out=mean[:, :n], in0=ssq[:, :n], scalar1=1.0 / D, scalar2=EPS,
                     op0=ALU.mult, op1=ALU.add,
                 )
-                rstd = stats.tile([P, STATS_TILES], F32)
                 nc.gpsimd.tensor_tensor(
                     out=rstd[:, :n], in0=mean[:, :n], in1=minus_half[:, :n], op=ALU.pow
                 )
-                for k in range(n):
-                    rstd_tiles[t + 1 - n + k] = rstd[:, k : k + 1]
+            for k in range(n):
+                rstd_tiles[t + 1 - n + k] = rstd[:, k : k + 1]
 
         for t in range(STATS_AHEAD):
             sum_squares(t)
@@ -211,12 +221,13 @@ def tile_attention_pa_t_kernel(tc, x, pre_norm_w, wq, wk, out_0, out_1):
         w_scales = consts.tile([P, PASSES, N_COLS], U8, align_bytes=64)
         w_banks = [transpose_words(w_words[:, e, :]) for e in range(2)]
 
-        def prepare_weights():
-            for e, w_bank in enumerate(w_banks):
-                nc.vector.tensor_copy(
-                    out=w_grouped_words[:, :, (1 - e) * DM : (2 - e) * DM, :],
-                    in_=w_bank[:].rearrange("p g u n -> p g n u"),
-                )
+        for e, w_bank in enumerate(w_banks):
+            nc.scalar.copy(
+                out=w_grouped_words[:, :, (1 - e) * DM : (2 - e) * DM, :],
+                in_=w_bank[:].rearrange("p g u n -> p g n u"),
+            )
+
+        def quantise_weights():
             nc.vector.quantize_mx(
                 out=w_codes[:].rearrange("p g c -> p (g c)").bitcast(FP8X4),
                 scales=w_scales[:].rearrange("p g c -> p (g c)"),
@@ -229,7 +240,7 @@ def tile_attention_pa_t_kernel(tc, x, pre_norm_w, wq, wk, out_0, out_1):
                 out=h[:], in0=x_tiles[t], scalar=rstd_tiles[t],
                 in1=gain[:], op0=ALU.mult, op1=ALU.mult,
             )
-            bank = transpose_words(h[:].bitcast(F32), warm_up=True)
+            bank = transpose_words(h[:].bitcast(F32))
             grouped = mx_pool.tile([P, PASSES, P, PACK], BF16, align_bytes=64)
             nc.scalar.copy(
                 out=grouped[:].bitcast(F32),
@@ -263,6 +274,14 @@ def tile_attention_pa_t_kernel(tc, x, pre_norm_w, wq, wk, out_0, out_1):
                     )
             acc_tiles[t] = acc
 
+        def on_gpsimd(t):
+            return t % GPSIMD_EVERY == GPSIMD_EVERY - 1 and 0 <= t < N_TILES - STORE_TILES // 2
+
+        def copy_for_gpsimd(t):
+            acc_sb = acc_pool.tile([P, 3 * DM], F32)
+            nc.scalar.copy(out=acc_sb[:], in_=acc_tiles[t][:, : 3 * DM])
+            acc_tiles[t] = acc_sb
+
         def rotate(t):
             last = t >= N_TILES - STORE_TILES // 2
             n_store = 1 if last else 2 if t >= N_TILES - STORE_TILES else STORE_TILES
@@ -274,7 +293,7 @@ def tile_attention_pa_t_kernel(tc, x, pre_norm_w, wq, wk, out_0, out_1):
             rotated_tiles[t] = rotated
             table = rope[:, t % SLOTS].unsqueeze(2).to_broadcast([P, 3, 2, PAIRS])
             product = rope_pool.tile([P, 3, 2, PAIRS], F32)
-            nc.vector.tensor_tensor(
+            (nc.gpsimd if on_gpsimd(t) else nc.vector).tensor_tensor(
                 out=product[:],
                 in0=acc_tiles[t][:, : 3 * DM].rearrange("p (e m j) -> p e m j", e=3, m=2),
                 in1=table, op=ALU.mult,
@@ -299,18 +318,20 @@ def tile_attention_pa_t_kernel(tc, x, pre_norm_w, wq, wk, out_0, out_1):
             if loaded < min(step + LOAD_AHEAD + LOAD_TILES, N_TILES):
                 load(loaded, LOAD_TILES)
                 loaded += LOAD_TILES
+            if on_gpsimd(step - ROTATE_BEHIND):
+                copy_for_gpsimd(step - ROTATE_BEHIND)
+            if step == 0:
+                normalise_and_transpose(step)
             if step + STATS_AHEAD < N_TILES:
                 sum_squares(step + STATS_AHEAD)
-            if step < N_TILES:
+            if 0 < step < N_TILES:
                 normalise_and_transpose(step)
-            if step == 0:
-                make_table(0)
-                prepare_weights()
             if step == 1:
-                make_table(1)
+                quantise_weights()
+            if step == 2:
                 reduce_angles(2, 3)
-            if step in (4, 8):
-                make_table(step // 4 + 1)
+            if step < SLOTS // TABLE_SLOTS:
+                make_table(step)
             catch_up = 1 if step >= N_TILES - 1 else 0
             while next_projected <= min(step - PROJECT_BEHIND + catch_up, N_TILES - 1):
                 quantise(next_projected)

import math
from contextlib import ExitStack

import concourse.mybir as mybir
from concourse.masks import make_identity

F32 = mybir.dt.float32
BF16 = mybir.dt.bfloat16
I32 = mybir.dt.int32
U32 = mybir.dt.uint32
U8 = mybir.dt.uint8
FP8X4 = mybir.dt.float8_e4m3fn_x4
ALU = mybir.AluOpType
ACT = mybir.ActivationFunctionType

BATCH, SEQ, D = 4, 2048, 1024
DM = 128
PAIRS = DM // 2
EPS = 1e-9
ROPE_BASE = 10000.0

P = 128
PACK = 4
PASSES = D // (P * PACK)
WORDS = D // 2
SLOTS = SEQ // P
N_TILES = BATCH * SLOTS
N_COLS = 2 * DM
BANK = 512
MATMUL_COLS = 512
STATS_TILES = 2
SINGLES = 4
TABLE_SLOTS = 4
LOAD_TILES = 4
STORE_TILES = 4
FIRST_SCALAR_RSTD = 6
GPSIMD_EVERY = 8
STATS_AHEAD = 3
PROJECT_BEHIND = 2
ROTATE_BEHIND = 3
LOAD_AHEAD = 8

ROUND_MAGIC = 12582912.0

FLOPS = 2 * BATCH * SEQ * D * 2 * DM


def tile_attention_pa_t_kernel(tc, x, pre_norm_w, wq, wk, out_0, out_1):
    nc = tc.nc
    x_rows = x.rearrange("b (p t) d -> b p t d", t=SLOTS)
    out_rows = [o.rearrange("b (p t) h n -> b p (t h n)", t=SLOTS) for o in (out_0, out_1)]
    with ExitStack() as ctx:
        ctx.enter_context(tc.manual_schedule())
        consts = ctx.enter_context(tc.tile_pool(name="consts", bufs=1))
        x_pool = ctx.enter_context(tc.tile_pool(name="x", bufs=SINGLES + 2))
        junk = ctx.enter_context(tc.tile_pool(name="junk", bufs=2))
        stats = ctx.enter_context(tc.tile_pool(name="stats", bufs=STATS_AHEAD + 2))
        h_pool = ctx.enter_context(tc.tile_pool(name="h", bufs=4))
        mx_pool = ctx.enter_context(tc.tile_pool(name="mx", bufs=4))
        rope_pool = ctx.enter_context(tc.tile_pool(name="rope", bufs=6))
        acc_pool = ctx.enter_context(tc.tile_pool(name="acc", bufs=2))
        out_pool = ctx.enter_context(tc.tile_pool(name="out", bufs=3))
        psum_g = ctx.enter_context(tc.psum_pool(name="psum_g", bufs=1))
        psum_t = ctx.enter_context(tc.psum_pool(name="psum_t", bufs=3))
        psum_o = ctx.enter_context(tc.psum_pool(name="psum_o", bufs=4))

        x_tiles, ssq_tiles, rstd_tiles = {}, {}, {}
        grouped_tiles, code_tiles, scale_tiles = {}, {}, {}
        acc_tiles, rotated_tiles = {}, {}

        def load(first, n):
            x_sb = x_pool.tile([P, LOAD_TILES, D], BF16)
            slot = first % SLOTS
            nc.sync.dma_start(out=x_sb[:, :n], in_=x_rows[first // SLOTS, :, slot : slot + n, :])
            for i in range(n):
                x_tiles[first + i] = x_sb[:, i, :]

        gain_row = consts.tile([P, D], BF16)
        nc.vector.memset(gain_row[:], 0.0)
        load(0, 1)
        load(1, 1)
        nc.sync.dma_start(out=gain_row[0:1, :], in_=pre_norm_w.rearrange("(o d) -> o d", o=1))
        w_rows = consts.tile([P, 2, D], BF16)
        for m, w in enumerate((wq, wk)):
            nc.sync.dma_start(
                out=w_rows[m * PAIRS : (m + 1) * PAIRS, :, :], in_=w.rearrange("(j e) d -> j e d", e=2)
            )
        load(2, 1)
        load(3, 1)
        load(4, LOAD_TILES)
        position_int = consts.tile([P, SLOTS], I32)
        nc.gpsimd.iota(position_int[:], pattern=[[1, SLOTS]], base=0, channel_multiplier=SLOTS)
        ident = consts.tile([P, P], F32)
        make_identity(nc, ident[:])

        one = consts.tile([P, 1], F32)
        nc.vector.memset(one[:], 1.0)
        minus_half = consts.tile([P, STATS_TILES], F32)
        nc.vector.memset(minus_half[:], -0.5)
        warm = consts.tile([P, 1], F32)
        nc.scalar.activation(out=warm[:], in_=one[:], func=ACT.Sin)
        ones = consts.tile([P, P], BF16)
        nc.vector.memset(ones[:], 1.0)
        gain = psum_g.tile([P, D], BF16)
        for half in range(D // MATMUL_COLS):
            cols = slice(half * MATMUL_COLS, (half + 1) * MATMUL_COLS)
            nc.tensor.matmul(out=gain[:, cols], lhsT=ones[:], rhs=gain_row[:, cols], start=True, stop=True)
        eps = consts.tile([P, 1], F32)
        nc.vector.tensor_scalar(out=eps[:], in0=one[:], scalar1=EPS, scalar2=None, op0=ALU.mult)
        quarter_turn = consts.tile([P, 1], F32)
        nc.vector.tensor_scalar(
            out=quarter_turn[:], in0=one[:], scalar1=math.pi / 2, scalar2=None, op0=ALU.mult
        )

        turns_per_step = consts.tile([P, PAIRS], F32)
        n = 8
        for j in range(n):
            nc.vector.tensor_scalar(
                out=turns_per_step[:, j : j + 1], in0=one[:],
                scalar1=ROPE_BASE ** (-j / PAIRS) / (2 * math.pi), scalar2=None, op0=ALU.mult,
            )
        while n < PAIRS:
            nc.vector.tensor_scalar(
                out=turns_per_step[:, n : 2 * n], in0=turns_per_step[:, 0:n],
                scalar1=ROPE_BASE ** (-n / PAIRS), scalar2=None, op0=ALU.mult,
            )
            n *= 2
        position = consts.tile([P, SLOTS], F32)
        nc.vector.tensor_copy(out=position[:], in_=position_int[:])
        turns = consts.tile([P, SLOTS, PAIRS], F32)
        shifted = consts.tile([P, SLOTS, PAIRS], F32)
        neg_frac = consts.tile([P, SLOTS, PAIRS], F32)
        abs_frac = consts.tile([P, SLOTS, PAIRS], F32)
        sin = consts.tile([P, SLOTS, PAIRS], F32)
        rope = consts.tile([P, SLOTS, 3, PAIRS], F32)

        def reduce_angles(*chunks):
            slots = [slice(c * TABLE_SLOTS, (c + 1) * TABLE_SLOTS) for c in chunks]
            shape = [P, TABLE_SLOTS, PAIRS]
            for s in slots:
                nc.vector.tensor_tensor(
                    out=turns[:, s],
                    in0=position[:, s].unsqueeze(2).to_broadcast(shape),
                    in1=turns_per_step[:].unsqueeze(1).to_broadcast(shape),
                    op=ALU.mult,
                )
            for s in slots:
                nc.vector.tensor_scalar(
                    out=shifted[:, s], in0=turns[:, s], scalar1=ROUND_MAGIC, scalar2=None, op0=ALU.add
                )
            for s in slots:
                nc.vector.scalar_tensor_tensor(
                    out=neg_frac[:, s], in0=shifted[:, s], scalar=ROUND_MAGIC, in1=turns[:, s],
                    op0=ALU.subtract, op1=ALU.subtract,
                )
            for s in slots:
                nc.vector.scalar_tensor_tensor(
                    out=abs_frac[:, s], in0=neg_frac[:, s], scalar=-1.0, in1=neg_frac[:, s],
                    op0=ALU.mult, op1=ALU.max,
                )

        def make_table(chunk):
            lo, hi = chunk * TABLE_SLOTS, (chunk + 1) * TABLE_SLOTS
            cos = rope[:, lo:hi, 2, :]
            nc.scalar.activation(
                out=cos, in_=abs_frac[:, lo:hi], func=ACT.Sin, bias=quarter_turn[:], scale=-2 * math.pi
            )
            nc.scalar.activation(
                out=sin[:, lo:hi], in_=neg_frac[:, lo:hi], func=ACT.Sin, scale=-2 * math.pi
            )
            nc.gpsimd.tensor_tensor(out=rope[:, lo:hi, 0, :], in0=cos, in1=sin[:, lo:hi], op=ALU.add)
            nc.gpsimd.tensor_tensor(out=rope[:, lo:hi, 1, :], in0=cos, in1=sin[:, lo:hi], op=ALU.subtract)

        reduce_angles(0, 1)

        def transpose_words(words):
            bank = psum_t.tile([P, PASSES, 2, P], F32)
            for c in range(WORDS // P):
                nc.tensor.transpose(bank[:, c // 2, c % 2, :], words[:, c * P : (c + 1) * P], ident[:])
            return bank

        def sum_squares(t):
            n = 1 if t < SINGLES else STATS_TILES
            i = t % n
            if i == 0:
                ssq = stats.tile([P, STATS_TILES], F32)
            else:
                ssq = ssq_tiles[t - 1]
            ssq_tiles[t] = ssq
            squares = junk.tile([P, D], BF16)
            nc.scalar.activation(
                out=squares[:], in_=x_tiles[t], func=ACT.Square, accum_out=ssq[:, i : i + 1]
            )
            if i + 1 < n:
                return
            rstd = stats.tile([P, STATS_TILES], F32)
            if t >= FIRST_SCALAR_RSTD:
                nc.scalar.activation(
                    out=rstd[:, :n], in_=ssq[:, :n], func=ACT.Abs_reciprocal_sqrt,
                    bias=eps[:], scale=1.0 / D,
                )
            else:
                mean = stats.tile([P, STATS_TILES], F32)
                nc.gpsimd.tensor_scalar(
                    out=mean[:, :n], in0=ssq[:, :n], scalar1=1.0 / D, scalar2=EPS,
                    op0=ALU.mult, op1=ALU.add,
                )
                nc.gpsimd.tensor_tensor(
                    out=rstd[:, :n], in0=mean[:, :n], in1=minus_half[:, :n], op=ALU.pow
                )
            for k in range(n):
                rstd_tiles[t + 1 - n + k] = rstd[:, k : k + 1]

        for t in range(STATS_AHEAD):
            sum_squares(t)

        w_grouped = consts.tile([P, PASSES, N_COLS, PACK], BF16, align_bytes=64)
        w_grouped_words = w_grouped[:].bitcast(F32)
        w_words = w_rows[:].bitcast(F32)
        w_codes = consts.tile([P, PASSES, N_COLS], U32, align_bytes=64)
        w_scales = consts.tile([P, PASSES, N_COLS], U8, align_bytes=64)
        w_banks = [transpose_words(w_words[:, e, :]) for e in range(2)]

        for e, w_bank in enumerate(w_banks):
            nc.scalar.copy(
                out=w_grouped_words[:, :, (1 - e) * DM : (2 - e) * DM, :],
                in_=w_bank[:].rearrange("p g u n -> p g n u"),
            )

        def quantise_weights():
            nc.vector.quantize_mx(
                out=w_codes[:].rearrange("p g c -> p (g c)").bitcast(FP8X4),
                scales=w_scales[:].rearrange("p g c -> p (g c)"),
                in_=w_grouped[:].rearrange("p g c t -> p (g c t)"),
            )

        def normalise_and_transpose(t):
            h = h_pool.tile([P, D], BF16)
            nc.vector.scalar_tensor_tensor(
                out=h[:], in0=x_tiles[t], scalar=rstd_tiles[t],
                in1=gain[:], op0=ALU.mult, op1=ALU.mult,
            )
            bank = transpose_words(h[:].bitcast(F32))
            grouped = mx_pool.tile([P, PASSES, P, PACK], BF16, align_bytes=64)
            nc.scalar.copy(
                out=grouped[:].bitcast(F32),
                in_=bank[:].rearrange("p g u k -> p g k u"),
            )
            grouped_tiles[t] = grouped

        def quantise(t):
            codes = mx_pool.tile([P, PASSES, P], U32, align_bytes=64)
            scales = mx_pool.tile([P, PASSES, P], U8, align_bytes=64)
            nc.vector.quantize_mx(
                out=codes[:].rearrange("p g k -> p (g k)").bitcast(FP8X4),
                scales=scales[:].rearrange("p g k -> p (g k)"),
                in_=grouped_tiles[t][:].rearrange("p g k t -> p (g k t)"),
            )
            code_tiles[t], scale_tiles[t] = codes, scales

        def project(t):
            acc = psum_o.tile([P, BANK], F32)
            for first_col, windows in (0, [(0, N_COLS)]), (N_COLS, [(0, DM), (DM, N_COLS)]):
                passes = [(g, lo, hi) for g in range(PASSES) for lo, hi in windows]
                for k, (g, lo, hi) in enumerate(passes):
                    nc.tensor.matmul_mx(
                        out=acc[:, first_col : first_col + hi - lo],
                        lhsT=code_tiles[t][:, g, :].bitcast(FP8X4),
                        lhsT_scale=scale_tiles[t][:, g, :],
                        rhs=w_codes[:, g, lo:hi].bitcast(FP8X4),
                        rhs_scale=w_scales[:, g, lo:hi],
                        start=(k == 0),
                        stop=(k == len(passes) - 1),
                    )
            acc_tiles[t] = acc

        def on_gpsimd(t):
            return t % GPSIMD_EVERY == GPSIMD_EVERY - 1 and 0 <= t < N_TILES - STORE_TILES // 2

        def copy_for_gpsimd(t):
            acc_sb = acc_pool.tile([P, 3 * DM], F32)
            nc.scalar.copy(out=acc_sb[:], in_=acc_tiles[t][:, : 3 * DM])
            acc_tiles[t] = acc_sb

        def rotate(t):
            last = t >= N_TILES - STORE_TILES // 2
            n_store = 1 if last else 2 if t >= N_TILES - STORE_TILES else STORE_TILES
            i = t % n_store
            if i == 0:
                rotated = out_pool.tile([P, 2, STORE_TILES, DM], F32)
            else:
                rotated = rotated_tiles[t - 1]
            rotated_tiles[t] = rotated
            table = rope[:, t % SLOTS].unsqueeze(2).to_broadcast([P, 3, 2, PAIRS])
            product = rope_pool.tile([P, 3, 2, PAIRS], F32)
            (nc.gpsimd if on_gpsimd(t) else nc.vector).tensor_tensor(
                out=product[:],
                in0=acc_tiles[t][:, : 3 * DM].rearrange("p (e m j) -> p e m j", e=3, m=2),
                in1=table, op=ALU.mult,
            )
            (nc.vector if last else nc.gpsimd).tensor_tensor(
                out=rotated[:, :, i, :].rearrange("p m (j e) -> p m j e", e=2),
                in0=product[:, 2].unsqueeze(3).to_broadcast([P, 2, PAIRS, 2]),
                in1=product[:, 0:2].rearrange("p e m j -> p m j e"),
                op=ALU.subtract,
            )
            if i + 1 == n_store:
                slot = t % SLOTS - i
                for m in range(2):
                    nc.sync.dma_start(
                        out=out_rows[m][t // SLOTS, :, slot * DM : (slot + n_store) * DM],
                        in_=rotated[:, m, :n_store].rearrange("p i n -> p (i n)"),
                    )

        loaded = SINGLES + LOAD_TILES
        next_projected, next_rotated = 0, 0
        for step in range(N_TILES + 2):
            if loaded < min(step + LOAD_AHEAD + LOAD_TILES, N_TILES):
                load(loaded, LOAD_TILES)
                loaded += LOAD_TILES
            if on_gpsimd(step - ROTATE_BEHIND):
                copy_for_gpsimd(step - ROTATE_BEHIND)
            if step == 0:
                normalise_and_transpose(step)
            if step + STATS_AHEAD < N_TILES:
                sum_squares(step + STATS_AHEAD)
            if 0 < step < N_TILES:
                normalise_and_transpose(step)
            if step == 1:
                quantise_weights()
            if step == 2:
                reduce_angles(2, 3)
            if step < SLOTS // TABLE_SLOTS:
                make_table(step)
            catch_up = 1 if step >= N_TILES - 1 else 0
            while next_projected <= min(step - PROJECT_BEHIND + catch_up, N_TILES - 1):
                quantise(next_projected)
                project(next_projected)
                next_projected += 1
            while next_rotated <= step - ROTATE_BEHIND + catch_up:
                rotate(next_rotated)
                next_rotated += 1
